import numpy as np
import ml_dtypes


def mxq(x, axis, fmt="e4m3"):
    dtype, down = {"e4m3": (ml_dtypes.float8_e4m3fn, 7), "e5m2": (ml_dtypes.float8_e5m2, 14)}[fmt]
    v = np.moveaxis(np.asarray(x, np.float32).astype(ml_dtypes.bfloat16).astype(np.float64), axis, -1)
    blocks = v.reshape(v.shape[:-1] + (-1, 32))
    amax = np.abs(blocks).max(-1, keepdims=True)
    byte = np.maximum(np.where(amax > 0, np.frexp(amax)[1] - 1 + 127, 0) - down, 1)
    scale = np.exp2(byte - 127.0)
    codes = (blocks / scale).astype(np.float32).astype(dtype).astype(np.float64)
    return np.moveaxis((codes * scale).reshape(v.shape), -1, axis)


WIDE = False


def mx_kscale(k):
    if not WIDE:
        return np.ones(k)
    levels = np.array([10, -10, 5, -5, 0])
    a = np.random.permutation(np.resize(levels, k // 512 * 4)).reshape(k // 512, 4)
    idx = np.arange(k)
    return np.exp2(a[idx // 512, idx % 128 // 32])


BF16 = ml_dtypes.bfloat16


def bf(x):
    return np.asarray(x, np.float32).astype(BF16)


def f64(x):
    return np.asarray(x).astype(np.float64)


B, S, D, H = 8, 512, 512, 4
HD = D // H
NEG_INF = -1e30


def alibi_causal_mask():
    i = np.arange(S)[:, None]
    j = np.arange(S)[None, :]
    return np.where(j <= i, -f64(i - j), NEG_INF)


def setup_inputs():
    t = mx_kscale(D)
    return {"q": bf(np.random.standard_normal((B, H, S, HD)) * 1.5),
            "k": bf(np.random.standard_normal((B, H, S, HD)) * 1.5),
            "v": bf(np.random.standard_normal((B, H, S, HD)) * 1.5 * t.reshape(H, 1, HD)),
            "w_out": bf(np.random.standard_normal((D, D)) / np.sqrt(D) / t[None, :]),
            "b_out": bf(np.random.standard_normal(D) * 0.1)}


def reference(q, k, v, w_out, b_out):
    s = f64(q) @ f64(k).transpose(0, 1, 3, 2) / np.sqrt(HD) + alibi_causal_mask()
    e = np.exp(s - s.max(-1, keepdims=True))
    o = (mxq(e, 3, "e4m3") @ mxq(f64(v), 2, "e4m3")) / e.sum(-1, keepdims=True)
    a = o.transpose(0, 2, 1, 3).reshape(B, S, D)
    return (mxq(a, 2, "e4m3") @ mxq(f64(w_out), 1, "e4m3").T) + f64(b_out)

@@ -1,0 +1,240 @@
+import math
+from contextlib import ExitStack
+
+import concourse.mybir as mybir
+from concourse.masks import make_identity
+
+F32 = mybir.dt.float32
+BF16 = mybir.dt.bfloat16
+I32 = mybir.dt.int32
+U32 = mybir.dt.uint32
+U8 = mybir.dt.uint8
+FP8X4 = mybir.dt.float8_e4m3fn_x4
+ALU = mybir.AluOpType
+FUNC = mybir.ActivationFunctionType
+AXIS = mybir.AxisListType
+
+B, H, S, HD = 8, 4, 512, 128
+D = H * HD
+P = 128
+PACK = 4
+TILES = S // P
+HALF = S // 2
+NEG_INF = -1e30
+E_BUFS = 3
+
+FLOPS = 2 * (2 * B * H * S * S * HD) + 2 * B * S * D * D
+
+
+def words_to_mx(nc, pools, ident_f32, words, keep):
+    grouped = pools["stage"].tile([P, TILES, P, PACK], BF16, align_bytes=64)
+    grouped_words = grouped[:].bitcast(F32)
+    for first in range(0, TILES, 2):
+        turned = pools["psum_words"].tile([P, 2, 2, P], F32)
+        for t in range(2):
+            for u in range(2):
+                nc.tensor.transpose(turned[:, t, u, :], words[:, first + t, u, :], ident_f32[:])
+        nc.scalar.copy(
+            out=grouped_words[:, first : first + 2, :, :],
+            in_=turned[:].rearrange("p t u r -> p t r u"),
+        )
+    codes = keep.tile([P, TILES * P], U32, align_bytes=64)
+    scales = keep.tile([P, TILES * P], U8, align_bytes=64)
+    nc.vector.quantize_mx(
+        out=codes[:].bitcast(FP8X4),
+        scales=scales[:],
+        in_=grouped[:].rearrange("p t r c -> p (t r c)"),
+    )
+    return codes, scales
+
+
+def tile_alibiattention_pa_t_kernel(tc, q, k, v, w_out, b_out, out):
+    nc = tc.nc
+    with ExitStack() as stack:
+        pools = {
+            name: stack.enter_context(tc.tile_pool(name=name, bufs=bufs))
+            for name, bufs in (
+                ("consts", 1),
+                ("rows", 3),
+                ("turned_qk", 3),
+                ("scores", 4),
+                ("stats", 3),
+                ("stage", 3),
+                ("mx_v", 2),
+                ("mx_e", 3),
+                ("mx_a", 2),
+                ("result", 2),
+            )
+        }
+        for name, bufs in (
+            ("psum_qk", 1),
+            ("psum_scores", 3),
+            ("psum_words", 2),
+            ("psum_heads", 1),
+            ("psum_out", 1),
+        ):
+            pools[name] = stack.enter_context(tc.psum_pool(name=name, bufs=bufs))
+        consts = pools["consts"]
+
+        ident_bf16 = consts.tile([P, P], BF16)
+        make_identity(nc, ident_bf16[:])
+        ident_f32 = consts.tile([P, P], F32)
+        make_identity(nc, ident_f32[:])
+
+        distance = consts.tile([P, 2, P, 2], I32)
+        nc.gpsimd.iota(
+            distance[:], pattern=[[2, 2], [PACK, P], [1, 2]], base=-(S - P), channel_multiplier=-1
+        )
+        alibi = consts.tile([P, 2, HALF], F32)
+        nc.vector.tensor_copy(out=alibi[:], in_=distance[:].rearrange("r u p x -> r u (p x)"))
+        future = consts.tile([P, 2, HALF], F32)
+        nc.vector.tensor_scalar(
+            out=future[:], in0=alibi[:], scalar1=0.0, scalar2=NEG_INF, op0=ALU.is_gt, op1=ALU.mult
+        )
+        nc.vector.tensor_tensor(out=alibi[:], in0=alibi[:], in1=future[:], op=ALU.add)
+
+        e_rows_ring = [
+            consts.tile([P, TILES, 2, HALF], BF16, name="e_rows%d" % i) for i in range(E_BUFS)
+        ]
+        for e_rows in e_rows_ring:
+            nc.vector.memset(e_rows[:], 0.0)
+
+        def load_sequence(b):
+            q_rows = pools["rows"].tile([P, H * TILES, HD], BF16)
+            nc.sync.dma_start(out=q_rows[:], in_=q[b].rearrange("h (t r) d -> r (h t) d", r=P))
+            k_rows = pools["rows"].tile([P, H * TILES, HD], BF16)
+            nc.sync.dma_start(out=k_rows[:], in_=k[b].rearrange("h (t r) d -> r (h t) d", r=P))
+            v_rows = pools["rows"].tile([P, H, PACK, HD], BF16)
+            nc.sync.dma_start(out=v_rows[:], in_=v[b].rearrange("h (p c) d -> p h c d", c=PACK))
+            return q_rows, k_rows, v_rows
+
+        loaded = load_sequence(0)
+        w_rows = consts.tile([P, TILES, D], BF16)
+        nc.sync.dma_start(out=w_rows[:], in_=w_out.rearrange("(t r) c -> r t c", r=P))
+        bias = consts.tile([P, D], BF16)
+        nc.sync.dma_start(out=bias[:], in_=b_out.partition_broadcast(P))
+        w_codes, w_scales = words_to_mx(
+            nc,
+            pools,
+            ident_f32,
+            w_rows[:].bitcast(F32).rearrange("r t (p u) -> r t u p", u=2),
+            consts,
+        )
+
+        for b in range(B):
+            q_rows, k_rows, v_rows = loaded
+            if b + 1 < B:
+                loaded = load_sequence(b + 1)
+
+            v_grouped = pools["stage"].tile([P, H, HD, PACK], BF16, align_bytes=64)
+            nc.vector.tensor_copy(out=v_grouped[:], in_=v_rows[:].rearrange("p h c d -> p h d c"))
+            v_codes = pools["mx_v"].tile([P, H * HD], U32, align_bytes=64)
+            v_scales = pools["mx_v"].tile([P, H * HD], U8, align_bytes=64)
+            nc.vector.quantize_mx(
+                out=v_codes[:].bitcast(FP8X4),
+                scales=v_scales[:],
+                in_=v_grouped[:].rearrange("p h d c -> p (h d c)"),
+            )
+
+            a_rows = pools["mx_a"].tile([P, TILES, D], BF16)
+            for h in range(H):
+                head_cols = slice(h * HD, (h + 1) * HD)
+
+                qk_turned = pools["psum_qk"].tile([P, 2, S], BF16)
+                for which, rows in enumerate((q_rows, k_rows)):
+                    for t in range(TILES):
+                        nc.tensor.transpose(
+                            qk_turned[:, which, t * P : (t + 1) * P],
+                            rows[:, h * TILES + t, :],
+                            ident_bf16[:],
+                        )
+                q_t = pools["turned_qk"].tile([P, S], BF16)
+                nc.scalar.copy(out=q_t[:], in_=qk_turned[:, 0, :])
+                k_t = pools["turned_qk"].tile([P, 2, HALF], BF16)
+                nc.scalar.copy(
+                    out=k_t[:].bitcast(F32),
+                    in_=qk_turned[:].bitcast(F32)[:, 1, :].rearrange("d (p u) -> d u p", u=2),
+                )
+
+                e_rows = e_rows_ring[(b * H + h) % E_BUFS]
+                neg_max = pools["stats"].tile([P, TILES], F32)
+                row_sum = pools["stats"].tile([P, TILES], F32)
+                for t in range(TILES):
+                    n = (t + 1) * P // 2
+                    s_sums = pools["psum_scores"].tile([P, 2, HALF], F32)
+                    nc.tensor.matmul(
+                        s_sums[:, :, :n],
+                        lhsT=q_t[:, t * P : (t + 1) * P],
+                        rhs=k_t[:, :, :n],
+                        start=True,
+                        stop=True,
+                    )
+                    s = pools["scores"].tile([P, 2, HALF], F32)
+                    nc.vector.scalar_tensor_tensor(
+                        out=s[:, :, :n],
+                        in0=s_sums[:, :, :n],
+                        scalar=1.0 / math.sqrt(HD),
+                        in1=alibi[:, :, HALF - n :],
+                        op0=ALU.mult,
+                        op1=ALU.add,
+                    )
+                    nc.vector.tensor_reduce(
+                        out=neg_max[:, t : t + 1], in_=s[:, :, :n], axis=AXIS.XY, op=ALU.max, negate=True
+                    )
+                    nc.scalar.activation(
+                        out=e_rows[:, t, :, :n],
+                        in_=s[:, :, :n],
+                        func=FUNC.Exp,
+                        bias=neg_max[:, t : t + 1],
+                        scale=1.0,
+                        accum_out=row_sum[:, t : t + 1],
+                    )
+                one_over_sum = pools["stats"].tile([P, TILES], F32)
+                nc.vector.reciprocal(out=one_over_sum[:], in_=row_sum[:])
+
+                e_codes, e_scales = words_to_mx(
+                    nc, pools, ident_f32, e_rows[:].bitcast(F32), pools["mx_e"]
+                )
+
+                o_sums = pools["psum_heads"].tile([P, TILES, HD], F32)
+                for t in range(TILES):
+                    tile_cols = slice(t * P, (t + 1) * P)
+                    nc.tensor.matmul_mx(
+                        out=o_sums[:, t, :],
+                        lhsT=e_codes[:, tile_cols].bitcast(FP8X4),
+                        lhsT_scale=e_scales[:, tile_cols],
+                        rhs=v_codes[:, head_cols].bitcast(FP8X4),
+                        rhs_scale=v_scales[:, head_cols],
+                        start=True,
+                        stop=True,
+                    )
+                for t in range(TILES):
+                    nc.scalar.activation(
+                        out=a_rows[:, t, head_cols],
+                        in_=o_sums[:, t, :],
+                        func=FUNC.Copy,
+                        scale=one_over_sum[:, t : t + 1],
+                    )
+
+            a_codes, a_scales = words_to_mx(
+                nc,
+                pools,
+                ident_f32,
+                a_rows[:].bitcast(F32).rearrange("r t (p u) -> r t u p", u=2),
+                pools["mx_a"],
+            )
+            result = pools["result"].tile([P, TILES, D], F32)
+            for t in range(TILES):
+                tile_cols = slice(t * P, (t + 1) * P)
+                out_sums = pools["psum_out"].tile([P, D], F32)
+                nc.tensor.matmul_mx(
+                    out=out_sums[:],
+                    lhsT=a_codes[:, tile_cols].bitcast(FP8X4),
+                    lhsT_scale=a_scales[:, tile_cols],
+                    rhs=w_codes[:].bitcast(FP8X4),
+                    rhs_scale=w_scales[:],
+                    start=True,
+                    stop=True,
+                )
+                nc.vector.tensor_tensor(out=result[:, t, :], in0=out_sums[:], in1=bias[:], op=ALU.add)
+            nc.sync.dma_start(out=out[b].rearrange("(t r) n -> r t n", r=P), in_=result[:])

@@ -20,32 +20,11 @@ P = 128
 PACK = 4
 TILES = S // P
 HALF = S // 2
+HEADS = B * H
 NEG_INF = -1e30
-E_BUFS = 3
+E_RING = 3
 
 FLOPS = 2 * (2 * B * H * S * S * HD) + 2 * B * S * D * D
-
-
-def words_to_mx(nc, pools, ident_f32, words, keep):
-    grouped = pools["stage"].tile([P, TILES, P, PACK], BF16, align_bytes=64)
-    grouped_words = grouped[:].bitcast(F32)
-    for first in range(0, TILES, 2):
-        turned = pools["psum_words"].tile([P, 2, 2, P], F32)
-        for t in range(2):
-            for u in range(2):
-                nc.tensor.transpose(turned[:, t, u, :], words[:, first + t, u, :], ident_f32[:])
-        nc.scalar.copy(
-            out=grouped_words[:, first : first + 2, :, :],
-            in_=turned[:].rearrange("p t u r -> p t r u"),
-        )
-    codes = keep.tile([P, TILES * P], U32, align_bytes=64)
-    scales = keep.tile([P, TILES * P], U8, align_bytes=64)
-    nc.vector.quantize_mx(
-        out=codes[:].bitcast(FP8X4),
-        scales=scales[:],
-        in_=grouped[:].rearrange("p t r c -> p (t r c)"),
-    )
-    return codes, scales
 
 
 def tile_alibiattention_pa_t_kernel(tc, q, k, v, w_out, b_out, out):
@@ -55,15 +34,16 @@ def tile_alibiattention_pa_t_kernel(tc, q, k, v, w_out, b_out, out):
             name: stack.enter_context(tc.tile_pool(name=name, bufs=bufs))
             for name, bufs in (
                 ("consts", 1),
-                ("rows", 3),
+                ("rows", 2),
                 ("turned_qk", 3),
-                ("scores", 4),
-                ("stats", 3),
-                ("stage", 3),
-                ("mx_v", 2),
+                ("scores", 6),
+                ("stats", 4),
+                ("stage", 2),
                 ("mx_e", 3),
-                ("mx_a", 2),
-                ("result", 2),
+                ("mx_v", 4),
+                ("a_rows", 3),
+                ("mx_a", 3),
+                ("result", 4),
             )
         }
         for name, bufs in (
@@ -81,6 +61,17 @@ def tile_alibiattention_pa_t_kernel(tc, q, k, v, w_out, b_out, out):
         ident_f32 = consts.tile([P, P], F32)
         make_identity(nc, ident_f32[:])
 
+        zero = consts.tile([P, 1], F32)
+        nc.vector.memset(zero[:], 0.0)
+        one = consts.tile([P, 1], F32)
+        nc.scalar.activation(out=one[:], in_=zero[:], func=FUNC.Exp)
+
+        e_rows_ring = [
+            consts.tile([P, TILES, 2, HALF], BF16, name="e_rows%d" % i) for i in range(E_RING)
+        ]
+        for e_rows in e_rows_ring:
+            nc.vector.memset(e_rows[:], 0.0)
+
         distance = consts.tile([P, 2, P, 2], I32)
         nc.gpsimd.iota(
             distance[:], pattern=[[2, 2], [PACK, P], [1, 2]], base=-(S - P), channel_multiplier=-1
@@ -93,148 +84,242 @@ def tile_alibiattention_pa_t_kernel(tc, q, k, v, w_out, b_out, out):
         )
         nc.vector.tensor_tensor(out=alibi[:], in0=alibi[:], in1=future[:], op=ALU.add)
 
-        e_rows_ring = [
-            consts.tile([P, TILES, 2, HALF], BF16, name="e_rows%d" % i) for i in range(E_BUFS)
-        ]
-        for e_rows in e_rows_ring:
-            nc.vector.memset(e_rows[:], 0.0)
+        def turn_words(words, grouped_words):
+            tiles = words.shape[1]
+            turned = pools["psum_words"].tile([P, tiles, 2, P], F32)
+            for t in range(tiles):
+                for u in range(2):
+                    nc.tensor.transpose(turned[:, t, u, :], words[:, t, u, :], ident_f32[:])
+            nc.scalar.copy(out=grouped_words, in_=turned[:].rearrange("p t u r -> p t r u"))
+
+        def quantise(grouped, keep):
+            columns = grouped.shape[1]
+            codes = keep.tile([P, columns], U32, align_bytes=64)
+            scales = keep.tile([P, columns], U8, align_bytes=64)
+            nc.vector.quantize_mx(
+                out=codes[:].bitcast(FP8X4), scales=scales[:], in_=grouped.rearrange("p n c -> p (n c)")
+            )
+            return codes, scales
+
+        seq_rows = {}
+        turned_qk = {}
+        scores = {}
+        stats = {}
+        inverse_sums = {}
+        grouped_e, grouped_v, grouped_a = {}, {}, {}
+        mx_e, mx_v, mx_a = {}, {}, {}
+        a_rows = {}
 
         def load_sequence(b):
+            if b >= B:
+                return
             q_rows = pools["rows"].tile([P, H * TILES, HD], BF16)
             nc.sync.dma_start(out=q_rows[:], in_=q[b].rearrange("h (t r) d -> r (h t) d", r=P))
             k_rows = pools["rows"].tile([P, H * TILES, HD], BF16)
             nc.sync.dma_start(out=k_rows[:], in_=k[b].rearrange("h (t r) d -> r (h t) d", r=P))
             v_rows = pools["rows"].tile([P, H, PACK, HD], BF16)
             nc.sync.dma_start(out=v_rows[:], in_=v[b].rearrange("h (p c) d -> p h c d", c=PACK))
-            return q_rows, k_rows, v_rows
+            seq_rows[b] = (q_rows, k_rows, v_rows)
 
-        loaded = load_sequence(0)
+        def turn_qk(g):
+            if g >= HEADS:
+                return
+            b, h = divmod(g, H)
+            qk_turned = pools["psum_qk"].tile([P, 2, S], BF16)
+            for which in range(2):
+                for t in range(TILES):
+                    nc.tensor.transpose(
+                        qk_turned[:, which, t * P : (t + 1) * P],
+                        seq_rows[b][which][:, h * TILES + t, :],
+                        ident_bf16[:],
+                    )
+            q_t = pools["turned_qk"].tile([P, S], BF16)
+            nc.scalar.copy(out=q_t[:], in_=qk_turned[:, 0, :])
+            k_t = pools["turned_qk"].tile([P, 2, HALF], BF16)
+            nc.scalar.copy(
+                out=k_t[:].bitcast(F32),
+                in_=qk_turned[:].bitcast(F32)[:, 1, :].rearrange("d (p u) -> d u p", u=2),
+            )
+            turned_qk[g] = (q_t, k_t)
+
+        def plane_columns(t):
+            return (t + 1) * P // 2
+
+        def score_tile(g, t):
+            if g >= HEADS:
+                return
+            q_t, k_t = turned_qk[g]
+            n = plane_columns(t)
+            s_sums = pools["psum_scores"].tile([P, 2, HALF], F32)
+            nc.tensor.matmul(
+                s_sums[:, :, :n], lhsT=q_t[:, t * P : (t + 1) * P], rhs=k_t[:, :, :n], start=True, stop=True
+            )
+            s = pools["scores"].tile([P, 2, HALF], F32)
+            nc.vector.scalar_tensor_tensor(
+                out=s[:, :, :n],
+                in0=s_sums[:, :, :n],
+                scalar=1.0 / math.sqrt(HD),
+                in1=alibi[:, :, HALF - n :],
+                op0=ALU.mult,
+                op1=ALU.add,
+            )
+            scores[g, t] = s
+
+        def soften_tile(g, t):
+            if g >= HEADS:
+                return
+            if t == 0:
+                neg_max = pools["stats"].tile([P, TILES], F32)
+                row_sum = pools["stats"].tile([P, TILES], F32)
+                stats[g] = (neg_max, row_sum)
+            neg_max, row_sum = stats[g]
+            n = plane_columns(t)
+            s = scores[g, t]
+            nc.vector.tensor_reduce(
+                out=neg_max[:, t : t + 1], in_=s[:, :, :n], axis=AXIS.XY, op=ALU.max, negate=True
+            )
+            nc.scalar.activation(
+                out=e_rows_ring[g % E_RING][:, t, :, :n],
+                in_=s[:, :, :n],
+                func=FUNC.Exp,
+                bias=neg_max[:, t : t + 1],
+                scale=1.0,
+                accum_out=row_sum[:, t : t + 1],
+            )
+
+        def invert_sums(g):
+            if not 0 <= g < HEADS:
+                return
+            one_over_sum = pools["stats"].tile([P, TILES], F32)
+            nc.vector.reciprocal(out=one_over_sum[:], in_=stats[g][1][:])
+            inverse_sums[g] = one_over_sum
+
+        def turn_e(g, first):
+            if not 0 <= g < HEADS:
+                return
+            if first == 0:
+                grouped_e[g] = pools["stage"].tile(
+                    [P, TILES, P, PACK], BF16, align_bytes=64, name="grouped_e"
+                )
+            turn_words(
+                e_rows_ring[g % E_RING][:].bitcast(F32)[:, first : first + 2],
+                grouped_e[g][:].bitcast(F32)[:, first : first + 2],
+            )
+
+        def quantise_e(g):
+            if not 0 <= g < HEADS:
+                return
+            mx_e[g] = quantise(grouped_e[g][:].rearrange("p t r c -> p (t r) c"), pools["mx_e"])
+
+        def group_v(g):
+            if g >= HEADS:
+                return
+            b, h = divmod(g, H)
+            grouped_v[g] = pools["stage"].tile([P, HD, PACK], BF16, align_bytes=64, name="grouped_v")
+            nc.vector.tensor_copy(
+                out=grouped_v[g][:], in_=seq_rows[b][2][:, h, :, :].rearrange("p c d -> p d c")
+            )
+
+        def quantise_v(g):
+            if g >= HEADS:
+                return
+            mx_v[g] = quantise(grouped_v[g][:], pools["mx_v"])
+
+        def e_times_v(g):
+            if not 0 <= g < HEADS:
+                return
+            b, h = divmod(g, H)
+            if h == 0:
+                a_rows[b] = pools["a_rows"].tile([P, TILES, D], BF16, name="a_rows")
+            e_codes, e_scales = mx_e[g]
+            v_codes, v_scales = mx_v[g]
+            o_sums = pools["psum_heads"].tile([P, TILES, HD], F32)
+            for t in range(TILES):
+                tile_cols = slice(t * P, (t + 1) * P)
+                nc.tensor.matmul_mx(
+                    out=o_sums[:, t, :],
+                    lhsT=e_codes[:, tile_cols].bitcast(FP8X4),
+                    lhsT_scale=e_scales[:, tile_cols],
+                    rhs=v_codes[:].bitcast(FP8X4),
+                    rhs_scale=v_scales[:],
+                    start=True,
+                    stop=True,
+                )
+            for t in range(TILES):
+                nc.scalar.activation(
+                    out=a_rows[b][:, t, h * HD : (h + 1) * HD],
+                    in_=o_sums[:, t, :],
+                    func=FUNC.Copy,
+                    scale=inverse_sums[g][:, t : t + 1],
+                )
+
+        def turn_a(y):
+            if not 0 <= y < B * TILES:
+                return
+            b, t = divmod(y, TILES)
+            grouped_a[y] = pools["stage"].tile([P, 1, P, PACK], BF16, align_bytes=64, name="grouped_a")
+            turn_words(
+                a_rows[b][:].bitcast(F32).rearrange("r t (p u) -> r t u p", u=2)[:, t : t + 1],
+                grouped_a[y][:].bitcast(F32),
+            )
+
+        def quantise_a(y):
+            if not 0 <= y < B * TILES:
+                return
+            mx_a[y] = quantise(grouped_a[y][:].rearrange("p t r c -> p (t r) c"), pools["mx_a"])
+
+        def project(y):
+            if not 0 <= y < B * TILES:
+                return
+            b, t = divmod(y, TILES)
+            a_codes, a_scales = mx_a[y]
+            out_sums = pools["psum_out"].tile([P, D], F32)
+            nc.tensor.matmul_mx(
+                out=out_sums[:],
+                lhsT=a_codes[:].bitcast(FP8X4),
+                lhsT_scale=a_scales[:],
+                rhs=w_codes[:].bitcast(FP8X4),
+                rhs_scale=w_scales[:],
+                start=True,
+                stop=True,
+            )
+            result = pools["result"].tile([P, D], F32)
+            nc.vector.tensor_tensor(out=result[:], in0=out_sums[:], in1=bias[:], op=ALU.add)
+            nc.sync.dma_start(out=out[b, t * P : (t + 1) * P, :], in_=result[:])
+
         w_rows = consts.tile([P, TILES, D], BF16)
         nc.sync.dma_start(out=w_rows[:], in_=w_out.rearrange("(t r) c -> r t c", r=P))
         bias = consts.tile([P, D], BF16)
         nc.sync.dma_start(out=bias[:], in_=b_out.partition_broadcast(P))
-        w_codes, w_scales = words_to_mx(
-            nc,
-            pools,
-            ident_f32,
-            w_rows[:].bitcast(F32).rearrange("r t (p u) -> r t u p", u=2),
-            consts,
-        )
-
-        for b in range(B):
-            q_rows, k_rows, v_rows = loaded
-            if b + 1 < B:
-                loaded = load_sequence(b + 1)
-
-            v_grouped = pools["stage"].tile([P, H, HD, PACK], BF16, align_bytes=64)
-            nc.vector.tensor_copy(out=v_grouped[:], in_=v_rows[:].rearrange("p h c d -> p h d c"))
-            v_codes = pools["mx_v"].tile([P, H * HD], U32, align_bytes=64)
-            v_scales = pools["mx_v"].tile([P, H * HD], U8, align_bytes=64)
-            nc.vector.quantize_mx(
-                out=v_codes[:].bitcast(FP8X4),
-                scales=v_scales[:],
-                in_=v_grouped[:].rearrange("p h d c -> p (h d c)"),
+        load_sequence(0)
+        grouped_w = consts.tile([P, TILES, P, PACK], BF16, align_bytes=64)
+        for first in range(0, TILES, 2):
+            turn_words(
+                w_rows[:].bitcast(F32).rearrange("r t (p u) -> r t u p", u=2)[:, first : first + 2],
+                grouped_w[:].bitcast(F32)[:, first : first + 2],
             )
+        w_codes, w_scales = quantise(grouped_w[:].rearrange("p t r c -> p (t r) c"), consts)
+        turn_qk(0)
 
-            a_rows = pools["mx_a"].tile([P, TILES, D], BF16)
-            for h in range(H):
-                head_cols = slice(h * HD, (h + 1) * HD)
-
-                qk_turned = pools["psum_qk"].tile([P, 2, S], BF16)
-                for which, rows in enumerate((q_rows, k_rows)):
-                    for t in range(TILES):
-                        nc.tensor.transpose(
-                            qk_turned[:, which, t * P : (t + 1) * P],
-                            rows[:, h * TILES + t, :],
-                            ident_bf16[:],
-                        )
-                q_t = pools["turned_qk"].tile([P, S], BF16)
-                nc.scalar.copy(out=q_t[:], in_=qk_turned[:, 0, :])
-                k_t = pools["turned_qk"].tile([P, 2, HALF], BF16)
-                nc.scalar.copy(
-                    out=k_t[:].bitcast(F32),
-                    in_=qk_turned[:].bitcast(F32)[:, 1, :].rearrange("d (p u) -> d u p", u=2),
-                )
-
-                e_rows = e_rows_ring[(b * H + h) % E_BUFS]
-                neg_max = pools["stats"].tile([P, TILES], F32)
-                row_sum = pools["stats"].tile([P, TILES], F32)
-                for t in range(TILES):
-                    n = (t + 1) * P // 2
-                    s_sums = pools["psum_scores"].tile([P, 2, HALF], F32)
-                    nc.tensor.matmul(
-                        s_sums[:, :, :n],
-                        lhsT=q_t[:, t * P : (t + 1) * P],
-                        rhs=k_t[:, :, :n],
-                        start=True,
-                        stop=True,
-                    )
-                    s = pools["scores"].tile([P, 2, HALF], F32)
-                    nc.vector.scalar_tensor_tensor(
-                        out=s[:, :, :n],
-                        in0=s_sums[:, :, :n],
-                        scalar=1.0 / math.sqrt(HD),
-                        in1=alibi[:, :, HALF - n :],
-                        op0=ALU.mult,
-                        op1=ALU.add,
-                    )
-                    nc.vector.tensor_reduce(
-                        out=neg_max[:, t : t + 1], in_=s[:, :, :n], axis=AXIS.XY, op=ALU.max, negate=True
-                    )
-                    nc.scalar.activation(
-                        out=e_rows[:, t, :, :n],
-                        in_=s[:, :, :n],
-                        func=FUNC.Exp,
-                        bias=neg_max[:, t : t + 1],
-                        scale=1.0,
-                        accum_out=row_sum[:, t : t + 1],
-                    )
-                one_over_sum = pools["stats"].tile([P, TILES], F32)
-                nc.vector.reciprocal(out=one_over_sum[:], in_=row_sum[:])
-
-                e_codes, e_scales = words_to_mx(
-                    nc, pools, ident_f32, e_rows[:].bitcast(F32), pools["mx_e"]
-                )
-
-                o_sums = pools["psum_heads"].tile([P, TILES, HD], F32)
-                for t in range(TILES):
-                    tile_cols = slice(t * P, (t + 1) * P)
-                    nc.tensor.matmul_mx(
-                        out=o_sums[:, t, :],
-                        lhsT=e_codes[:, tile_cols].bitcast(FP8X4),
-                        lhsT_scale=e_scales[:, tile_cols],
-                        rhs=v_codes[:, head_cols].bitcast(FP8X4),
-                        rhs_scale=v_scales[:, head_cols],
-                        start=True,
-                        stop=True,
-                    )
-                for t in range(TILES):
-                    nc.scalar.activation(
-                        out=a_rows[:, t, head_cols],
-                        in_=o_sums[:, t, :],
-                        func=FUNC.Copy,
-                        scale=one_over_sum[:, t : t + 1],
-                    )
-
-            a_codes, a_scales = words_to_mx(
-                nc,
-                pools,
-                ident_f32,
-                a_rows[:].bitcast(F32).rearrange("r t (p u) -> r t u p", u=2),
-                pools["mx_a"],
-            )
-            result = pools["result"].tile([P, TILES, D], F32)
-            for t in range(TILES):
-                tile_cols = slice(t * P, (t + 1) * P)
-                out_sums = pools["psum_out"].tile([P, D], F32)
-                nc.tensor.matmul_mx(
-                    out=out_sums[:],
-                    lhsT=a_codes[:, tile_cols].bitcast(FP8X4),
-                    lhsT_scale=a_scales[:, tile_cols],
-                    rhs=w_codes[:].bitcast(FP8X4),
-                    rhs_scale=w_scales[:],
-                    start=True,
-                    stop=True,
-                )
-                nc.vector.tensor_tensor(out=result[:, t, :], in0=out_sums[:], in1=bias[:], op=ALU.add)
-            nc.sync.dma_start(out=out[b].rearrange("(t r) n -> r t n", r=P), in_=result[:])
+        for g in range(HEADS + 7):
+            if g % H == 0:
+                load_sequence(g // H + 1)
+            score_tile(g, 0)
+            score_tile(g, 1)
+            project(g - 7)
+            e_times_v(g - 2)
+            invert_sums(g - 1)
+            soften_tile(g, 0)
+            turn_e(g - 1, 0)
+            score_tile(g, 2)
+            soften_tile(g, 1)
+            turn_e(g - 1, 2)
+            score_tile(g, 3)
+            soften_tile(g, 2)
+            turn_qk(g + 1)
+            turn_a(g - 6)
+            group_v(g)
+            soften_tile(g, 3)
+            quantise_e(g - 1)
+            quantise_v(g)
+            quantise_a(g - 6)

@@ -30,6 +30,7 @@ FLOPS = 2 * (2 * B * H * S * S * HD) + 2 * B * S * D * D
 def tile_alibiattention_pa_t_kernel(tc, q, k, v, w_out, b_out, out):
     nc = tc.nc
     with ExitStack() as stack:
+        stack.enter_context(tc.manual_schedule())
         pools = {
             name: stack.enter_context(tc.tile_pool(name=name, bufs=bufs))
             for name, bufs in (
@@ -304,22 +305,22 @@ def tile_alibiattention_pa_t_kernel(tc, q, k, v, w_out, b_out, out):
         for g in range(HEADS + 7):
             if g % H == 0:
                 load_sequence(g // H + 1)
+            turn_e(g - 1, 0)
             score_tile(g, 0)
             score_tile(g, 1)
-            project(g - 7)
-            e_times_v(g - 2)
-            invert_sums(g - 1)
             soften_tile(g, 0)
-            turn_e(g - 1, 0)
             score_tile(g, 2)
-            soften_tile(g, 1)
             turn_e(g - 1, 2)
+            soften_tile(g, 1)
+            e_times_v(g - 2)
             score_tile(g, 3)
             soften_tile(g, 2)
             turn_qk(g + 1)
             turn_a(g - 6)
             group_v(g)
             soften_tile(g, 3)
+            project(g - 7)
+            invert_sums(g - 1)
             quantise_e(g - 1)
             quantise_v(g)
             quantise_a(g - 6)

@@ -30,7 +30,6 @@ FLOPS = 2 * (2 * B * H * S * S * HD) + 2 * B * S * D * D
 def tile_alibiattention_pa_t_kernel(tc, q, k, v, w_out, b_out, out):
     nc = tc.nc
     with ExitStack() as stack:
-        stack.enter_context(tc.manual_schedule())
         pools = {
             name: stack.enter_context(tc.tile_pool(name=name, bufs=bufs))
             for name, bufs in (
@@ -129,10 +128,12 @@ def tile_alibiattention_pa_t_kernel(tc, q, k, v, w_out, b_out, out):
             qk_turned = pools["psum_qk"].tile([P, 2, S], BF16)
             for which in range(2):
                 for t in range(TILES):
-                    nc.tensor.transpose(
+                    nc.tensor.matmul(
                         qk_turned[:, which, t * P : (t + 1) * P],
-                        seq_rows[b][which][:, h * TILES + t, :],
-                        ident_bf16[:],
+                        lhsT=seq_rows[b][which][:, h * TILES + t, :],
+                        rhs=ident_bf16[:],
+                        start=True,
+                        stop=True,
                     )
             q_t = pools["turned_qk"].tile([P, S], BF16)
             nc.scalar.copy(out=q_t[:], in_=qk_turned[:, 0, :])
@@ -305,22 +306,22 @@ def tile_alibiattention_pa_t_kernel(tc, q, k, v, w_out, b_out, out):
         for g in range(HEADS + 7):
             if g % H == 0:
                 load_sequence(g // H + 1)
-            turn_e(g - 1, 0)
             score_tile(g, 0)
             score_tile(g, 1)
-            soften_tile(g, 0)
-            score_tile(g, 2)
-            turn_e(g - 1, 2)
-            soften_tile(g, 1)
+            project(g - 7)
             e_times_v(g - 2)
+            invert_sums(g - 1)
+            soften_tile(g, 0)
+            turn_e(g - 1, 0)
+            score_tile(g, 2)
+            soften_tile(g, 1)
+            turn_e(g - 1, 2)
             score_tile(g, 3)
             soften_tile(g, 2)
             turn_qk(g + 1)
             turn_a(g - 6)
             group_v(g)
             soften_tile(g, 3)
-            project(g - 7)
-            invert_sums(g - 1)
             quantise_e(g - 1)
             quantise_v(g)
             quantise_a(g - 6)

@@ -20,77 +20,151 @@ P = 128
 PACK = 4
 TILES = S // P
 HALF = S // 2
-HEADS = B * H
+Q_PARTS = P // PACK
+UNITS = B * TILES
 NEG_INF = -1e30
-E_RING = 3
+ROOT = math.sqrt(HD)
+
+QUADRANT = ((0, 1, 2, 3), (2, 3, 1, 0), (1, 0, 2, 3), (3, 2, 1, 0))
+SETS = (1, 2, 4, 4)
+SEQ_JOBS = sum(SETS)
+JOBS = B * SEQ_JOBS
+PRODUCT_LAG = (6, 7, 6, 5)
+AHEAD = 6
 
 FLOPS = 2 * (2 * B * H * S * S * HD) + 2 * B * S * D * D
+
+
+def first_quadrant(h, t):
+    return min(QUADRANT[h][: t + 1])
+
+
+def last_job(n):
+    b, t = divmod(n, TILES)
+    return SEQ_JOBS * b + sum(SETS[: t + 1]) - 1
+
+
+def product_round(n):
+    return last_job(n) + PRODUCT_LAG[n % TILES]
 
 
 def tile_alibiattention_pa_t_kernel(tc, q, k, v, w_out, b_out, out):
     nc = tc.nc
     with ExitStack() as stack:
+        stack.enter_context(tc.manual_schedule())
         pools = {
             name: stack.enter_context(tc.tile_pool(name=name, bufs=bufs))
             for name, bufs in (
                 ("consts", 1),
-                ("rows", 2),
-                ("turned_qk", 3),
-                ("scores", 6),
-                ("stats", 4),
-                ("stage", 2),
-                ("mx_e", 3),
-                ("mx_v", 4),
+                ("rows_qk", 6),
+                ("rows_v", 3),
+                ("turned_q", 5),
+                ("turned_k", 3),
+                ("maxima", 4),
+                ("sums", 8),
+                ("e_rows", 4),
+                ("stage", 3),
+                ("stage_v", 2),
+                ("mx_e", 12),
+                ("mx_v", 2),
                 ("a_rows", 3),
-                ("mx_a", 3),
+                ("mx_a", 5),
                 ("result", 4),
             )
         }
-        for name, bufs in (
-            ("psum_qk", 1),
-            ("psum_scores", 3),
-            ("psum_words", 2),
-            ("psum_heads", 1),
-            ("psum_out", 1),
-        ):
+        for name, bufs in (("psum_scores", 4), ("psum_words", 2), ("psum_products", 2)):
             pools[name] = stack.enter_context(tc.psum_pool(name=name, bufs=bufs))
         consts = pools["consts"]
 
+        rows_qk, rows_v = {}, {}
+
+        def load_qk(n):
+            if n >= UNITS:
+                return
+            b, t = divmod(n, TILES)
+            rows = pools["rows_qk"].tile([P, 2, H, HD], BF16)
+            for which, source in enumerate((q, k)):
+                nc.sync.dma_start(
+                    out=rows[:, which, :, :],
+                    in_=source[b, :, t * P : (t + 1) * P, :].rearrange("h r d -> r h d"),
+                )
+            rows_qk[n] = rows
+
+        def load_v(b):
+            if b >= B:
+                return
+            rows = pools["rows_v"].tile([P, H, PACK, HD], BF16)
+            for h in range(H):
+                m = 0
+                while m < TILES:
+                    after = m + 1
+                    while after < TILES and QUADRANT[h][after] == QUADRANT[h][after - 1] + 1:
+                        after += 1
+                    part = QUADRANT[h][m] * Q_PARTS
+                    nc.sync.dma_start(
+                        out=rows[part : part + (after - m) * Q_PARTS, h, :, :],
+                        in_=v[b, h, m * P : after * P, :].rearrange("(p c) d -> p c d", c=PACK),
+                    )
+                    m = after
+            rows_v[b] = rows
+
+        for n in range(AHEAD - 2):
+            load_qk(n)
+        load_v(0)
+        w_rows = consts.tile([P, TILES, D], BF16)
+        nc.sync.dma_start(out=w_rows[:], in_=w_out.rearrange("(t r) c -> r t c", r=P))
+        for n in range(AHEAD - 2, AHEAD + 1):
+            load_qk(n)
+        bias = consts.tile([P, D], BF16)
+        nc.sync.dma_start(out=bias[:], in_=b_out.partition_broadcast(P))
+        load_v(1)
+
         ident_bf16 = consts.tile([P, P], BF16)
         make_identity(nc, ident_bf16[:])
+        distance = consts.tile([P, TILES, P], I32)
+        nc.gpsimd.iota(distance[:], pattern=[[-P, TILES], [-1, P]], base=0, channel_multiplier=1)
         ident_f32 = consts.tile([P, P], F32)
         make_identity(nc, ident_f32[:])
+        alibi = consts.tile([P, TILES, P], F32)
+        nc.vector.tensor_copy(out=alibi[:], in_=distance[:])
+        nc.vector.tensor_scalar(out=alibi[:], in0=alibi[:], scalar1=ROOT, scalar2=None, op0=ALU.mult)
+        future = consts.tile([P, P], F32)
+        nc.vector.tensor_scalar(
+            out=future[:],
+            in0=alibi[:, 0, :],
+            scalar1=0.0,
+            scalar2=ROOT * NEG_INF,
+            op0=ALU.is_gt,
+            op1=ALU.mult,
+        )
+        nc.vector.tensor_tensor(out=alibi[:, 0, :], in0=alibi[:, 0, :], in1=future[:], op=ALU.add)
 
         zero = consts.tile([P, 1], F32)
         nc.vector.memset(zero[:], 0.0)
         one = consts.tile([P, 1], F32)
         nc.scalar.activation(out=one[:], in_=zero[:], func=FUNC.Exp)
 
-        e_rows_ring = [
-            consts.tile([P, TILES, 2, HALF], BF16, name="e_rows%d" % i) for i in range(E_RING)
-        ]
-        for e_rows in e_rows_ring:
-            nc.vector.memset(e_rows[:], 0.0)
+        e_rows_three = [consts.tile([P, 1, 2, HALF], BF16, name="e_rows_three%d" % h) for h in range(H)]
+        v_first = [consts.tile([P, H, HD], U32, align_bytes=64, name="v_first%d" % i) for i in range(2)]
+        v_two = [consts.tile([P, H, HD], U32, align_bytes=64, name="v_two%d" % i) for i in range(2)]
 
-        distance = consts.tile([P, 2, P, 2], I32)
-        nc.gpsimd.iota(
-            distance[:], pattern=[[2, 2], [PACK, P], [1, 2]], base=-(S - P), channel_multiplier=-1
-        )
-        alibi = consts.tile([P, 2, HALF], F32)
-        nc.vector.tensor_copy(out=alibi[:], in_=distance[:].rearrange("r u p x -> r u (p x)"))
-        future = consts.tile([P, 2, HALF], F32)
-        nc.vector.tensor_scalar(
-            out=future[:], in0=alibi[:], scalar1=0.0, scalar2=NEG_INF, op0=ALU.is_gt, op1=ALU.mult
-        )
-        nc.vector.tensor_tensor(out=alibi[:], in0=alibi[:], in1=future[:], op=ALU.add)
+        def lay_zeros():
+            for h in range(H):
+                low = QUADRANT[h][TILES - 1] * 2 * Q_PARTS
+                nc.vector.memset(e_rows_three[h][:, 0, :, low : low + 2 * Q_PARTS], 0.0)
+            for codes in v_first + v_two:
+                nc.vector.memset(codes[:].bitcast(I32), 0)
 
-        def turn_words(words, grouped_words):
+        def turn_words(words, pool, name):
             tiles = words.shape[1]
-            turned = pools["psum_words"].tile([P, tiles, 2, P], F32)
+            turned = pool.tile([P, tiles, 2, P], F32, name=name)
             for t in range(tiles):
                 for u in range(2):
                     nc.tensor.transpose(turned[:, t, u, :], words[:, t, u, :], ident_f32[:])
-            nc.scalar.copy(out=grouped_words, in_=turned[:].rearrange("p t u r -> p t r u"))
+            return turned
+
+        def group_words(turned, grouped):
+            nc.scalar.copy(out=grouped.bitcast(F32), in_=turned[:].rearrange("p t u r -> p t r u"))
 
         def quantise(grouped, keep):
             columns = grouped.shape[1]
@@ -101,227 +175,328 @@ def tile_alibiattention_pa_t_kernel(tc, q, k, v, w_out, b_out, out):
             )
             return codes, scales
 
-        seq_rows = {}
-        turned_qk = {}
-        scores = {}
-        stats = {}
-        inverse_sums = {}
-        grouped_e, grouped_v, grouped_a = {}, {}, {}
-        mx_e, mx_v, mx_a = {}, {}, {}
-        a_rows = {}
+        qk_products, turned_q, turned_k = {}, {}, {}
 
-        def load_sequence(b):
-            if b >= B:
+        def turn_qk(n, which):
+            if n >= UNITS:
                 return
-            q_rows = pools["rows"].tile([P, H * TILES, HD], BF16)
-            nc.sync.dma_start(out=q_rows[:], in_=q[b].rearrange("h (t r) d -> r (h t) d", r=P))
-            k_rows = pools["rows"].tile([P, H * TILES, HD], BF16)
-            nc.sync.dma_start(out=k_rows[:], in_=k[b].rearrange("h (t r) d -> r (h t) d", r=P))
-            v_rows = pools["rows"].tile([P, H, PACK, HD], BF16)
-            nc.sync.dma_start(out=v_rows[:], in_=v[b].rearrange("h (p c) d -> p h c d", c=PACK))
-            seq_rows[b] = (q_rows, k_rows, v_rows)
-
-        def turn_qk(g):
-            if g >= HEADS:
-                return
-            b, h = divmod(g, H)
-            qk_turned = pools["psum_qk"].tile([P, 2, S], BF16)
-            for which in range(2):
-                for t in range(TILES):
-                    nc.tensor.matmul(
-                        qk_turned[:, which, t * P : (t + 1) * P],
-                        lhsT=seq_rows[b][which][:, h * TILES + t, :],
-                        rhs=ident_bf16[:],
-                        start=True,
-                        stop=True,
-                    )
-            q_t = pools["turned_qk"].tile([P, S], BF16)
-            nc.scalar.copy(out=q_t[:], in_=qk_turned[:, 0, :])
-            k_t = pools["turned_qk"].tile([P, 2, HALF], BF16)
-            nc.scalar.copy(
-                out=k_t[:].bitcast(F32),
-                in_=qk_turned[:].bitcast(F32)[:, 1, :].rearrange("d (p u) -> d u p", u=2),
-            )
-            turned_qk[g] = (q_t, k_t)
-
-        def plane_columns(t):
-            return (t + 1) * P // 2
-
-        def score_tile(g, t):
-            if g >= HEADS:
-                return
-            q_t, k_t = turned_qk[g]
-            n = plane_columns(t)
-            s_sums = pools["psum_scores"].tile([P, 2, HALF], F32)
-            nc.tensor.matmul(
-                s_sums[:, :, :n], lhsT=q_t[:, t * P : (t + 1) * P], rhs=k_t[:, :, :n], start=True, stop=True
-            )
-            s = pools["scores"].tile([P, 2, HALF], F32)
-            nc.vector.scalar_tensor_tensor(
-                out=s[:, :, :n],
-                in0=s_sums[:, :, :n],
-                scalar=1.0 / math.sqrt(HD),
-                in1=alibi[:, :, HALF - n :],
-                op0=ALU.mult,
-                op1=ALU.add,
-            )
-            scores[g, t] = s
-
-        def soften_tile(g, t):
-            if g >= HEADS:
-                return
-            if t == 0:
-                neg_max = pools["stats"].tile([P, TILES], F32)
-                row_sum = pools["stats"].tile([P, TILES], F32)
-                stats[g] = (neg_max, row_sum)
-            neg_max, row_sum = stats[g]
-            n = plane_columns(t)
-            s = scores[g, t]
-            nc.vector.tensor_reduce(
-                out=neg_max[:, t : t + 1], in_=s[:, :, :n], axis=AXIS.XY, op=ALU.max, negate=True
-            )
-            nc.scalar.activation(
-                out=e_rows_ring[g % E_RING][:, t, :, :n],
-                in_=s[:, :, :n],
-                func=FUNC.Exp,
-                bias=neg_max[:, t : t + 1],
-                scale=1.0,
-                accum_out=row_sum[:, t : t + 1],
-            )
-
-        def invert_sums(g):
-            if not 0 <= g < HEADS:
-                return
-            one_over_sum = pools["stats"].tile([P, TILES], F32)
-            nc.vector.reciprocal(out=one_over_sum[:], in_=stats[g][1][:])
-            inverse_sums[g] = one_over_sum
-
-        def turn_e(g, first):
-            if not 0 <= g < HEADS:
-                return
-            if first == 0:
-                grouped_e[g] = pools["stage"].tile(
-                    [P, TILES, P, PACK], BF16, align_bytes=64, name="grouped_e"
-                )
-            turn_words(
-                e_rows_ring[g % E_RING][:].bitcast(F32)[:, first : first + 2],
-                grouped_e[g][:].bitcast(F32)[:, first : first + 2],
-            )
-
-        def quantise_e(g):
-            if not 0 <= g < HEADS:
-                return
-            mx_e[g] = quantise(grouped_e[g][:].rearrange("p t r c -> p (t r) c"), pools["mx_e"])
-
-        def group_v(g):
-            if g >= HEADS:
-                return
-            b, h = divmod(g, H)
-            grouped_v[g] = pools["stage"].tile([P, HD, PACK], BF16, align_bytes=64, name="grouped_v")
-            nc.vector.tensor_copy(
-                out=grouped_v[g][:], in_=seq_rows[b][2][:, h, :, :].rearrange("p c d -> p d c")
-            )
-
-        def quantise_v(g):
-            if g >= HEADS:
-                return
-            mx_v[g] = quantise(grouped_v[g][:], pools["mx_v"])
-
-        def e_times_v(g):
-            if not 0 <= g < HEADS:
-                return
-            b, h = divmod(g, H)
-            if h == 0:
-                a_rows[b] = pools["a_rows"].tile([P, TILES, D], BF16, name="a_rows")
-            e_codes, e_scales = mx_e[g]
-            v_codes, v_scales = mx_v[g]
-            o_sums = pools["psum_heads"].tile([P, TILES, HD], F32)
-            for t in range(TILES):
-                tile_cols = slice(t * P, (t + 1) * P)
-                nc.tensor.matmul_mx(
-                    out=o_sums[:, t, :],
-                    lhsT=e_codes[:, tile_cols].bitcast(FP8X4),
-                    lhsT_scale=e_scales[:, tile_cols],
-                    rhs=v_codes[:].bitcast(FP8X4),
-                    rhs_scale=v_scales[:],
+            if which == 0:
+                qk_products[n] = pools["psum_products"].tile([P, 2, H, P], BF16, name="product")
+            for h in range(H):
+                nc.tensor.matmul(
+                    qk_products[n][:, which, h, :],
+                    lhsT=rows_qk[n][:, which, h, :],
+                    rhs=ident_bf16[:],
                     start=True,
                     stop=True,
                 )
-            for t in range(TILES):
-                nc.scalar.activation(
-                    out=a_rows[b][:, t, h * HD : (h + 1) * HD],
-                    in_=o_sums[:, t, :],
-                    func=FUNC.Copy,
-                    scale=inverse_sums[g][:, t : t + 1],
+
+        def copy_qk(n):
+            if n >= UNITS:
+                return
+            b, t = divmod(n, TILES)
+            words = qk_products[n][:].rearrange("d w h r -> d w (h r)").bitcast(F32)
+            q_t = pools["turned_q"].tile([P, H, P], BF16)
+            nc.scalar.copy(out=q_t[:].rearrange("d h r -> d (h r)").bitcast(F32), in_=words[:, 0, :])
+            turned_q[n] = q_t
+            if t == 0:
+                turned_k[b] = pools["turned_k"].tile([P, H * TILES, P], BF16, name="k_t")
+            for h in range(0, H, 2):
+                place = [TILES * head + QUADRANT[head][t] for head in (h, h + 1)]
+                nc.scalar.copy(
+                    out=turned_k[b][:, place[0] : place[1] + 1 : place[1] - place[0], :].bitcast(F32),
+                    in_=words[:, 1, h * P // 2 : (h + 2) * P // 2].rearrange("d (h w) -> d h w", h=2),
                 )
 
-        def turn_a(y):
-            if not 0 <= y < B * TILES:
+        jobs = [(n, i) for n in range(UNITS) for i in range(SETS[n % TILES])]
+        scores, exp_biases, row_sums, e_rows, turned_e, grouped_e, mx_e = {}, {}, {}, {}, {}, {}, {}
+
+        def job_heads(j):
+            n, i = jobs[j]
+            heads = H // SETS[n % TILES]
+            return n, n % TILES, range(i * heads, (i + 1) * heads)
+
+        def score(j):
+            if not 0 <= j < JOBS:
                 return
-            b, t = divmod(y, TILES)
-            grouped_a[y] = pools["stage"].tile([P, 1, P, PACK], BF16, align_bytes=64, name="grouped_a")
-            turn_words(
-                a_rows[b][:].bitcast(F32).rearrange("r t (p u) -> r t u p", u=2)[:, t : t + 1],
-                grouped_a[y][:].bitcast(F32),
+            n, t, heads = job_heads(j)
+            keys = (t + 1) * P
+            k_t = turned_k[n // TILES][:].rearrange("d b j -> d (b j)")
+            s_sums = pools["psum_scores"].tile([P, S], F32)
+            for i, h in enumerate(heads):
+                low = first_quadrant(h, t)
+                nc.tensor.matmul(
+                    s_sums[:, i * keys : (i + 1) * keys],
+                    lhsT=turned_q[n][:, h, :],
+                    rhs=k_t[:, h * S + low * P : h * S + low * P + keys],
+                    start=True,
+                    stop=False,
+                )
+                for place in range(t + 1):
+                    m = QUADRANT[h].index(low + place)
+                    nc.tensor.matmul(
+                        s_sums[:, i * keys + place * P : i * keys + (place + 1) * P],
+                        lhsT=alibi[:, t - m, :],
+                        rhs=ident_f32[:],
+                        start=False,
+                        stop=place == t,
+                        is_transpose=True,
+                    )
+            scores[j] = s_sums
+
+        def row_max(j):
+            if not 0 <= j < JOBS:
+                return
+            n, t, heads = job_heads(j)
+            keys = (t + 1) * P
+            neg_max = pools["maxima"].tile([P, len(heads)], F32, name="neg_max")
+            nc.vector.tensor_reduce(
+                out=neg_max[:],
+                in_=scores[j][:, : len(heads) * keys].rearrange("r (h j) -> r h j", j=keys),
+                axis=AXIS.X,
+                op=ALU.max,
+                negate=True,
+            )
+            exp_bias = pools["maxima"].tile([P, len(heads)], F32, name="exp_bias")
+            nc.gpsimd.tensor_scalar(
+                out=exp_bias[:], in0=neg_max[:], scalar1=1.0 / ROOT, scalar2=0.0, op0=ALU.mult, op1=ALU.add
+            )
+            exp_biases[j] = exp_bias
+
+        def soften(j):
+            if not 0 <= j < JOBS:
+                return
+            n, t, heads = job_heads(j)
+            keys = (t + 1) * P
+            if heads[0] == 0:
+                row_sums[n] = pools["sums"].tile([P, H], F32, name="row_sum")
+            if t == 2:
+                e_rows[j] = e_rows_three[heads[0]]
+            else:
+                e_rows[j] = pools["e_rows"].tile([P, 1, 2, HALF], BF16, name="e_rows")
+            for i, h in enumerate(heads):
+                low = first_quadrant(h, t) * 2 * Q_PARTS
+                nc.scalar.activation(
+                    out=e_rows[j][:, 0, :, low : low + keys // 2].rearrange("r u (p x) -> r u p x", x=2),
+                    in_=scores[j][:, i * keys : (i + 1) * keys].rearrange(
+                        "r (p u x) -> r u p x", u=2, x=2
+                    ),
+                    func=FUNC.Exp,
+                    bias=exp_biases[j][:, i : i + 1],
+                    scale=1.0 / ROOT,
+                    accum_out=row_sums[n][:, h : h + 1],
+                )
+
+        def turn_e(j):
+            if not 0 <= j < JOBS:
+                return
+            turned_e[j] = turn_words(e_rows[j][:].bitcast(F32), pools["psum_words"], "turned_e")
+
+        def copy_e(j):
+            if not 0 <= j < JOBS:
+                return
+            grouped_e[j] = pools["stage"].tile([P, 1, P, PACK], BF16, align_bytes=64, name="grouped_e")
+            group_words(turned_e[j], grouped_e[j][:])
+
+        def quantise_e(j):
+            if not 0 <= j < JOBS:
+                return
+            mx_e[j] = quantise(grouped_e[j][:].rearrange("p t r c -> p (t r) c"), pools["mx_e"])
+
+        grouped_v, mx_v = {}, {}
+
+        def group_v(b, h, half):
+            if b >= B:
+                return
+            if h == 0 and half == 0:
+                grouped_v[b] = pools["stage_v"].tile(
+                    [P, H, HD, PACK], BF16, align_bytes=64, name="grouped_v"
+                )
+            part = slice(half * HD // 2, (half + 1) * HD // 2)
+            nc.gpsimd.tensor_scalar(
+                out=grouped_v[b][:, h, part, :],
+                in0=rows_v[b][:, h, :, part].rearrange("p c d -> p d c"),
+                scalar1=1.0,
+                scalar2=0.0,
+                op0=ALU.mult,
+                op1=ALU.add,
             )
 
-        def quantise_a(y):
-            if not 0 <= y < B * TILES:
+        def quantise_v(b):
+            if b >= B:
                 return
-            mx_a[y] = quantise(grouped_a[y][:].rearrange("p t r c -> p (t r) c"), pools["mx_a"])
+            mx_v[b] = quantise(grouped_v[b][:].rearrange("p h d c -> p (h d) c"), pools["mx_v"])
 
-        def project(y):
-            if not 0 <= y < B * TILES:
+        def move_v_two(b):
+            if b >= B:
                 return
-            b, t = divmod(y, TILES)
-            a_codes, a_scales = mx_a[y]
-            out_sums = pools["psum_out"].tile([P, D], F32)
+            codes = mx_v[b][0][:].rearrange("p (h d) -> p h d", h=H).bitcast(I32)
+            two = v_two[b % 2][:].bitcast(I32)
+            for low in range(2):
+                part = slice(low * P // 2, (low + 1) * P // 2)
+                nc.vector.tensor_copy(out=two[part, low::2, :], in_=codes[part, low::2, :])
+
+        def move_v_first(b):
+            if b >= B:
+                return
+            codes = mx_v[b][0][:].rearrange("p (h d) -> p h d", h=H).bitcast(I32)
+            one_block = v_first[b % 2][:].bitcast(I32)
+            for h in range(H):
+                low = QUADRANT[h][0] * Q_PARTS
+                part = slice(low, low + Q_PARTS)
+                nc.vector.tensor_copy(out=one_block[part, h, :], in_=codes[part, h, :])
+
+        heads_sums, inverse_sums, a_rows, turned_a, grouped_a, mx_a, out_sums = {}, {}, {}, {}, {}, {}, {}
+
+        def e_times_v(n):
+            if not 0 <= n < UNITS:
+                return
+            b, t = divmod(n, TILES)
+            v_codes, v_scales = mx_v[b]
+            if t == 0:
+                v_codes = v_first[b % 2][:].rearrange("p h d -> p (h d)")
+            elif t == 1:
+                v_codes = v_two[b % 2][:].rearrange("p h d -> p (h d)")
+            else:
+                v_codes = v_codes[:]
+            o_sums = pools["psum_products"].tile([P, D], F32, name="product")
+            width = D // SETS[t]
+            for i in range(SETS[t]):
+                e_codes, e_scales = mx_e[last_job(n) - SETS[t] + 1 + i]
+                v_cols = slice(i * width, (i + 1) * width)
+                nc.tensor.matmul_mx(
+                    out=o_sums[:, v_cols],
+                    lhsT=e_codes[:].bitcast(FP8X4),
+                    lhsT_scale=e_scales[:],
+                    rhs=v_codes[:, v_cols].bitcast(FP8X4),
+                    rhs_scale=v_scales[:, v_cols],
+                    start=True,
+                    stop=True,
+                )
+            heads_sums[n] = o_sums
+
+        def invert(n):
+            if not 0 <= n < UNITS:
+                return
+            inverse_sums[n] = pools["sums"].tile([P, H], F32, name="one_over_sum")
+            nc.vector.reciprocal(out=inverse_sums[n][:], in_=row_sums[n][:])
+
+        def normalise(n):
+            if not 0 <= n < UNITS:
+                return
+            a_rows[n] = pools["a_rows"].tile([P, 1, 2, HALF], BF16, name="a_rows")
+            for u in range(2):
+                nc.vector.tensor_tensor(
+                    out=a_rows[n][:, 0, u, :].rearrange("r (h p x) -> r h p x", h=H, x=2),
+                    in0=heads_sums[n][:].rearrange("r (h p u x) -> r u h p x", h=H, u=2, x=2)[:, u],
+                    in1=inverse_sums[n][:].unsqueeze(2).unsqueeze(3).to_broadcast([P, H, HD // PACK, 2]),
+                    op=ALU.mult,
+                )
+
+        def turn_a(n):
+            if not 0 <= n < UNITS:
+                return
+            turned_a[n] = turn_words(a_rows[n][:].bitcast(F32), pools["psum_words"], "turned_e")
+
+        def copy_a(n):
+            if not 0 <= n < UNITS:
+                return
+            grouped_a[n] = pools["stage"].tile([P, 1, P, PACK], BF16, align_bytes=64, name="grouped_a")
+            group_words(turned_a[n], grouped_a[n][:])
+
+        def quantise_a(n):
+            if not 0 <= n < UNITS:
+                return
+            mx_a[n] = quantise(grouped_a[n][:].rearrange("p t r c -> p (t r) c"), pools["mx_a"])
+
+        def project(n):
+            if not 0 <= n < UNITS:
+                return
+            a_codes, a_scales = mx_a[n]
+            out_sums[n] = pools["psum_products"].tile([P, D], F32, name="product")
             nc.tensor.matmul_mx(
-                out=out_sums[:],
+                out=out_sums[n][:],
                 lhsT=a_codes[:].bitcast(FP8X4),
                 lhsT_scale=a_scales[:],
-                rhs=w_codes[:].bitcast(FP8X4),
-                rhs_scale=w_scales[:],
+                rhs=w_codes[0][:].bitcast(FP8X4),
+                rhs_scale=w_scales[0][:],
                 start=True,
                 stop=True,
             )
+
+        def add_bias(n):
+            if not 0 <= n < UNITS:
+                return
+            b, t = divmod(n, TILES)
             result = pools["result"].tile([P, D], F32)
-            nc.vector.tensor_tensor(out=result[:], in0=out_sums[:], in1=bias[:], op=ALU.add)
+            nc.vector.tensor_tensor(out=result[:], in0=out_sums[n][:], in1=bias[:], op=ALU.add)
             nc.sync.dma_start(out=out[b, t * P : (t + 1) * P, :], in_=result[:])
 
-        w_rows = consts.tile([P, TILES, D], BF16)
-        nc.sync.dma_start(out=w_rows[:], in_=w_out.rearrange("(t r) c -> r t c", r=P))
-        bias = consts.tile([P, D], BF16)
-        nc.sync.dma_start(out=bias[:], in_=b_out.partition_broadcast(P))
-        load_sequence(0)
+        w_words = w_rows[:].bitcast(F32).rearrange("r t (p u) -> r t u p", u=2)
+        turned_w = {}
         grouped_w = consts.tile([P, TILES, P, PACK], BF16, align_bytes=64)
-        for first in range(0, TILES, 2):
-            turn_words(
-                w_rows[:].bitcast(F32).rearrange("r t (p u) -> r t u p", u=2)[:, first : first + 2],
-                grouped_w[:].bitcast(F32)[:, first : first + 2],
-            )
-        w_codes, w_scales = quantise(grouped_w[:].rearrange("p t r c -> p (t r) c"), consts)
-        turn_qk(0)
+        w_codes, w_scales = [], []
 
-        for g in range(HEADS + 7):
-            if g % H == 0:
-                load_sequence(g // H + 1)
-            score_tile(g, 0)
-            score_tile(g, 1)
-            project(g - 7)
-            e_times_v(g - 2)
-            invert_sums(g - 1)
-            soften_tile(g, 0)
-            turn_e(g - 1, 0)
-            score_tile(g, 2)
-            soften_tile(g, 1)
-            turn_e(g - 1, 2)
-            score_tile(g, 3)
-            soften_tile(g, 2)
-            turn_qk(g + 1)
-            turn_a(g - 6)
-            group_v(g)
-            soften_tile(g, 3)
-            quantise_e(g - 1)
-            quantise_v(g)
-            quantise_a(g - 6)
+        products = {product_round(n): n for n in range(-AHEAD, UNITS + 3)}
+        for r in range(min(products), JOBS + 18):
+            seq, step = divmod(r, SEQ_JOBS)
+            event = products.get(r)
+            score(r + 3)
+            turn_e(r - 1)
+            if r - 2 in products:
+                turn_a(products[r - 2])
+            if event is not None:
+                e_times_v(event)
+                project(event - 3)
+            if r - 1 in products:
+                turn_qk(products[r - 1] + AHEAD, 0)
+                turn_qk(products[r - 1] + AHEAD, 1)
+            if r in (1, 3):
+                turned_w[r] = turn_words(w_words[:, r - 1 : r + 1], pools["psum_products"], "product")
+
+            row_max(r + 2)
+            quantise_e(r - 3)
+            if r - 4 in products:
+                quantise_a(products[r - 4])
+            if r - 1 in products:
+                normalise(products[r - 1])
+                add_bias(products[r - 1] - 3)
+            for n in range(UNITS):
+                if last_job(n) == r - 1:
+                    invert(n)
+            if r == -2:
+                lay_zeros()
+            if r == 5:
+                codes, scales = quantise(grouped_w[:].rearrange("p t r c -> p (t r) c"), consts)
+                w_codes.append(codes)
+                w_scales.append(scales)
+            if r == 4:
+                quantise_v(0)
+                move_v_first(0)
+                move_v_two(0)
+            if r > 0 and step == 9:
+                quantise_v(seq + 1)
+            if r > SEQ_JOBS and step == 1:
+                move_v_two(seq)
+            if r > SEQ_JOBS and step == 4:
+                move_v_first(seq)
+
+            if 0 <= r < 4:
+                group_v(0, r, 0)
+                group_v(0, r, 1)
+            if r >= 0 and step < 2 * H:
+                group_v(seq + 1, step // 2, step % 2)
+
+            soften(r)
+            copy_e(r - 2)
+            if r - 2 in products:
+                copy_qk(products[r - 2] + AHEAD)
+            if r - 3 in products:
+                copy_a(products[r - 3])
+            if r in (2, 4):
+                group_words(turned_w[r - 1], grouped_w[:, r - 2 : r])
+
+            if event is not None:
+                load_qk(event + 2 * AHEAD + 1)
+            if r >= 0 and step == 2:
+                load_v(seq + 2)

@@ -30,7 +30,9 @@ SETS = (1, 2, 4, 4)
 SEQ_JOBS = sum(SETS)
 JOBS = B * SEQ_JOBS
 PRODUCT_LAG = (6, 7, 6, 5)
-AHEAD = 6
+LATER = 3
+LOADS_AHEAD = 4
+TURN_STEPS = ((-8, -7), (-5, -4), (-3, -2), (0, 1))
 
 FLOPS = 2 * (2 * B * H * S * S * HD) + 2 * B * S * D * D
 
@@ -42,6 +44,10 @@ def first_quadrant(h, t):
 def last_job(n):
     b, t = divmod(n, TILES)
     return SEQ_JOBS * b + sum(SETS[: t + 1]) - 1
+
+
+def turn_round(n, which):
+    return SEQ_JOBS * (n // TILES) + TURN_STEPS[n % TILES][which]
 
 
 def product_round(n):
@@ -108,13 +114,12 @@ def tile_alibiattention_pa_t_kernel(tc, q, k, v, w_out, b_out, out):
                     m = after
             rows_v[b] = rows
 
-        for n in range(AHEAD - 2):
+        for n in range(LOADS_AHEAD - 1):
             load_qk(n)
         load_v(0)
         w_rows = consts.tile([P, TILES, D], BF16)
         nc.sync.dma_start(out=w_rows[:], in_=w_out.rearrange("(t r) c -> r t c", r=P))
-        for n in range(AHEAD - 2, AHEAD + 1):
-            load_qk(n)
+        load_qk(LOADS_AHEAD - 1)
         bias = consts.tile([P, D], BF16)
         nc.sync.dma_start(out=bias[:], in_=b_out.partition_broadcast(P))
         load_v(1)
@@ -178,71 +183,77 @@ def tile_alibiattention_pa_t_kernel(tc, q, k, v, w_out, b_out, out):
         qk_products, turned_q, turned_k = {}, {}, {}
 
         def turn_qk(n, which):
-            if n >= UNITS:
+            if not 0 <= n < UNITS:
                 return
-            if which == 0:
-                qk_products[n] = pools["psum_products"].tile([P, 2, H, P], BF16, name="product")
+            qk_products[n, which] = pools["psum_products"].tile([P, H, P], BF16, name="product")
             for h in range(H):
                 nc.tensor.matmul(
-                    qk_products[n][:, which, h, :],
+                    qk_products[n, which][:, h, :],
                     lhsT=rows_qk[n][:, which, h, :],
                     rhs=ident_bf16[:],
                     start=True,
                     stop=True,
                 )
 
-        def copy_qk(n):
-            if n >= UNITS:
+        def copy_qk(n, which):
+            if not 0 <= n < UNITS:
                 return
             b, t = divmod(n, TILES)
-            words = qk_products[n][:].rearrange("d w h r -> d w (h r)").bitcast(F32)
-            q_t = pools["turned_q"].tile([P, H, P], BF16)
-            nc.scalar.copy(out=q_t[:].rearrange("d h r -> d (h r)").bitcast(F32), in_=words[:, 0, :])
-            turned_q[n] = q_t
+            words = qk_products[n, which][:].rearrange("d h r -> d (h r)").bitcast(F32)
+            if which == 0:
+                turned_q[n] = pools["turned_q"].tile([P, H, P], BF16, name="q_t")
+                nc.scalar.copy(out=turned_q[n][:].rearrange("d h r -> d (h r)").bitcast(F32), in_=words)
+                return
             if t == 0:
                 turned_k[b] = pools["turned_k"].tile([P, H * TILES, P], BF16, name="k_t")
             for h in range(0, H, 2):
                 place = [TILES * head + QUADRANT[head][t] for head in (h, h + 1)]
                 nc.scalar.copy(
                     out=turned_k[b][:, place[0] : place[1] + 1 : place[1] - place[0], :].bitcast(F32),
-                    in_=words[:, 1, h * P // 2 : (h + 2) * P // 2].rearrange("d (h w) -> d h w", h=2),
+                    in_=words[:, h * P // 2 : (h + 2) * P // 2].rearrange("d (h w) -> d h w", h=2),
                 )
 
         jobs = [(n, i) for n in range(UNITS) for i in range(SETS[n % TILES])]
-        scores, exp_biases, row_sums, e_rows, turned_e, grouped_e, mx_e = {}, {}, {}, {}, {}, {}, {}
+        scores, neg_maxima, exp_biases, row_sums, e_rows, turned_e, grouped_e, mx_e = {}, {}, {}, {}, {}, {}, {}, {}
 
         def job_heads(j):
             n, i = jobs[j]
             heads = H // SETS[n % TILES]
             return n, n % TILES, range(i * heads, (i + 1) * heads)
 
-        def score(j):
+        def lay_mask(j):
+            if not 0 <= j < JOBS:
+                return
+            n, t, heads = job_heads(j)
+            keys = (t + 1) * P
+            scores[j] = pools["psum_scores"].tile([P, S], F32, name="s_sums")
+            for i, h in enumerate(heads):
+                for place in range(t + 1):
+                    m = QUADRANT[h].index(first_quadrant(h, t) + place)
+                    nc.tensor.matmul(
+                        scores[j][:, i * keys + place * P : i * keys + (place + 1) * P],
+                        lhsT=alibi[:, t - m, :],
+                        rhs=ident_f32[:],
+                        start=i == 0 and place == 0,
+                        stop=False,
+                        is_transpose=True,
+                    )
+
+        def add_scores(j):
             if not 0 <= j < JOBS:
                 return
             n, t, heads = job_heads(j)
             keys = (t + 1) * P
             k_t = turned_k[n // TILES][:].rearrange("d b j -> d (b j)")
-            s_sums = pools["psum_scores"].tile([P, S], F32)
             for i, h in enumerate(heads):
-                low = first_quadrant(h, t)
+                first = h * S + first_quadrant(h, t) * P
                 nc.tensor.matmul(
-                    s_sums[:, i * keys : (i + 1) * keys],
+                    scores[j][:, i * keys : (i + 1) * keys],
                     lhsT=turned_q[n][:, h, :],
-                    rhs=k_t[:, h * S + low * P : h * S + low * P + keys],
-                    start=True,
-                    stop=False,
+                    rhs=k_t[:, first : first + keys],
+                    start=False,
+                    stop=h == heads[-1],
                 )
-                for place in range(t + 1):
-                    m = QUADRANT[h].index(low + place)
-                    nc.tensor.matmul(
-                        s_sums[:, i * keys + place * P : i * keys + (place + 1) * P],
-                        lhsT=alibi[:, t - m, :],
-                        rhs=ident_f32[:],
-                        start=False,
-                        stop=place == t,
-                        is_transpose=True,
-                    )
-            scores[j] = s_sums
 
         def row_max(j):
             if not 0 <= j < JOBS:
@@ -257,11 +268,13 @@ def tile_alibiattention_pa_t_kernel(tc, q, k, v, w_out, b_out, out):
                 op=ALU.max,
                 negate=True,
             )
-            exp_bias = pools["maxima"].tile([P, len(heads)], F32, name="exp_bias")
-            nc.gpsimd.tensor_scalar(
-                out=exp_bias[:], in0=neg_max[:], scalar1=1.0 / ROOT, scalar2=0.0, op0=ALU.mult, op1=ALU.add
-            )
-            exp_biases[j] = exp_bias
+            neg_maxima[j] = neg_max
+
+        def scale_max(j):
+            if not 0 <= j < JOBS:
+                return
+            exp_biases[j] = pools["maxima"].tile([P, len(job_heads(j)[2])], F32, name="exp_bias")
+            nc.scalar.mul(exp_biases[j][:], neg_maxima[j][:], 1.0 / ROOT)
 
         def soften(j):
             if not 0 <= j < JOBS:
@@ -305,21 +318,15 @@ def tile_alibiattention_pa_t_kernel(tc, q, k, v, w_out, b_out, out):
 
         grouped_v, mx_v = {}, {}
 
-        def group_v(b, h, half):
+        def group_v(b, h):
             if b >= B:
                 return
-            if h == 0 and half == 0:
+            if h == 0:
                 grouped_v[b] = pools["stage_v"].tile(
                     [P, H, HD, PACK], BF16, align_bytes=64, name="grouped_v"
                 )
-            part = slice(half * HD // 2, (half + 1) * HD // 2)
-            nc.gpsimd.tensor_scalar(
-                out=grouped_v[b][:, h, part, :],
-                in0=rows_v[b][:, h, :, part].rearrange("p c d -> p d c"),
-                scalar1=1.0,
-                scalar2=0.0,
-                op0=ALU.mult,
-                op1=ALU.add,
+            nc.vector.tensor_copy(
+                out=grouped_v[b][:, h, :, :], in_=rows_v[b][:, h, :, :].rearrange("p c d -> p d c")
             )
 
         def quantise_v(b):
@@ -437,22 +444,25 @@ def tile_alibiattention_pa_t_kernel(tc, q, k, v, w_out, b_out, out):
         grouped_w = consts.tile([P, TILES, P, PACK], BF16, align_bytes=64)
         w_codes, w_scales = [], []
 
-        products = {product_round(n): n for n in range(-AHEAD, UNITS + 3)}
-        for r in range(min(products), JOBS + 18):
+        products = {product_round(n): n for n in range(UNITS + LATER)}
+        turns = {}
+        for n in range(UNITS):
+            for which in range(2):
+                turns[turn_round(n, which)] = (n, which)
+        for r in range(min(turns), JOBS + 18):
             seq, step = divmod(r, SEQ_JOBS)
-            event = products.get(r)
-            score(r + 3)
+            lay_mask(r + 3)
             turn_e(r - 1)
             if r - 2 in products:
                 turn_a(products[r - 2])
-            if event is not None:
-                e_times_v(event)
-                project(event - 3)
-            if r - 1 in products:
-                turn_qk(products[r - 1] + AHEAD, 0)
-                turn_qk(products[r - 1] + AHEAD, 1)
             if r in (1, 3):
                 turned_w[r] = turn_words(w_words[:, r - 1 : r + 1], pools["psum_products"], "product")
+            add_scores(r + 3)
+            if r in products:
+                e_times_v(products[r])
+                project(products[r] - LATER)
+            if r in turns:
+                turn_qk(*turns[r])
 
             row_max(r + 2)
             quantise_e(r - 3)
@@ -460,7 +470,7 @@ def tile_alibiattention_pa_t_kernel(tc, q, k, v, w_out, b_out, out):
                 quantise_a(products[r - 4])
             if r - 1 in products:
                 normalise(products[r - 1])
-                add_bias(products[r - 1] - 3)
+                add_bias(products[r - 1] - LATER)
             for n in range(UNITS):
                 if last_job(n) == r - 1:
                     invert(n)
@@ -480,23 +490,22 @@ def tile_alibiattention_pa_t_kernel(tc, q, k, v, w_out, b_out, out):
                 move_v_two(seq)
             if r > SEQ_JOBS and step == 4:
                 move_v_first(seq)
-
             if 0 <= r < 4:
-                group_v(0, r, 0)
-                group_v(0, r, 1)
-            if r >= 0 and step < 2 * H:
-                group_v(seq + 1, step // 2, step % 2)
+                group_v(0, r)
+            if r >= 0 and step % 2 == 0 and step < 2 * H:
+                group_v(seq + 1, step // 2)
 
+            scale_max(r + 1)
             soften(r)
             copy_e(r - 2)
-            if r - 2 in products:
-                copy_qk(products[r - 2] + AHEAD)
+            if r - 1 in turns:
+                copy_qk(*turns[r - 1])
             if r - 3 in products:
                 copy_a(products[r - 3])
             if r in (2, 4):
                 group_words(turned_w[r - 1], grouped_w[:, r - 2 : r])
 
-            if event is not None:
-                load_qk(event + 2 * AHEAD + 1)
+            if r in turns and turns[r][1] == 0:
+                load_qk(turns[r][0] + LOADS_AHEAD)
             if r >= 0 and step == 2:
                 load_v(seq + 2)

@@ -29,10 +29,12 @@ QUADRANT = ((0, 1, 2, 3), (2, 3, 1, 0), (1, 0, 2, 3), (3, 2, 1, 0))
 SETS = (1, 2, 4, 4)
 SEQ_JOBS = sum(SETS)
 JOBS = B * SEQ_JOBS
-PRODUCT_LAG = (6, 7, 6, 5)
+PAIRS = JOBS // 2
+PSUM_RINGS = (("psum_scores", 4), ("psum_words", 1), ("psum_products", 3))
+PRODUCT_LAG = 3
 LATER = 3
+TURN_LEAD = 3
 LOADS_AHEAD = 4
-TURN_STEPS = ((-8, -7), (-5, -4), (-3, -2), (0, 1))
 
 FLOPS = 2 * (2 * B * H * S * S * HD) + 2 * B * S * D * D
 
@@ -46,12 +48,29 @@ def last_job(n):
     return SEQ_JOBS * b + sum(SETS[: t + 1]) - 1
 
 
-def turn_round(n, which):
-    return SEQ_JOBS * (n // TILES) + TURN_STEPS[n % TILES][which]
+def v_round(b):
+    return last_job(TILES * b) // 2 + 2
 
 
-def product_round(n):
-    return last_job(n) + PRODUCT_LAG[n % TILES]
+def quantise_round(p):
+    return p + PRODUCT_LAG - (p >= PAIRS - 2)
+
+
+def product_rounds():
+    rounds = []
+    for n in range(UNITS):
+        earliest = quantise_round(last_job(n) // 2)
+        rounds.append(max(earliest, rounds[-1] + 1) if rounds else earliest)
+    return rounds
+
+
+def turn_rounds():
+    rounds = []
+    for n in reversed(range(UNITS)):
+        first_job = last_job(n) - SETS[n % TILES] + 1
+        latest = first_job // 2 - TURN_LEAD
+        rounds.append(min(latest, rounds[-1] - 1) if rounds else latest)
+    return rounds[::-1]
 
 
 def tile_alibiattention_pa_t_kernel(tc, q, k, v, w_out, b_out, out):
@@ -71,14 +90,14 @@ def tile_alibiattention_pa_t_kernel(tc, q, k, v, w_out, b_out, out):
                 ("e_rows", 4),
                 ("stage", 3),
                 ("stage_v", 2),
-                ("mx_e", 12),
+                ("mx_e", 8),
                 ("mx_v", 2),
                 ("a_rows", 3),
                 ("mx_a", 5),
                 ("result", 4),
             )
         }
-        for name, bufs in (("psum_scores", 4), ("psum_words", 2), ("psum_products", 2)):
+        for name, bufs in PSUM_RINGS:
             pools[name] = stack.enter_context(tc.psum_pool(name=name, bufs=bufs))
         consts = pools["consts"]
 
@@ -122,7 +141,6 @@ def tile_alibiattention_pa_t_kernel(tc, q, k, v, w_out, b_out, out):
         load_qk(LOADS_AHEAD - 1)
         bias = consts.tile([P, D], BF16)
         nc.sync.dma_start(out=bias[:], in_=b_out.partition_broadcast(P))
-        load_v(1)
 
         ident_bf16 = consts.tile([P, P], BF16)
         make_identity(nc, ident_bf16[:])
@@ -149,24 +167,20 @@ def tile_alibiattention_pa_t_kernel(tc, q, k, v, w_out, b_out, out):
         one = consts.tile([P, 1], F32)
         nc.scalar.activation(out=one[:], in_=zero[:], func=FUNC.Exp)
 
-        e_rows_three = [consts.tile([P, 1, 2, HALF], BF16, name="e_rows_three%d" % h) for h in range(H)]
+        e_rows_three = [consts.tile([P, 2, HALF], BF16, name="e_rows_three%d" % h) for h in range(H)]
         v_first = [consts.tile([P, H, HD], U32, align_bytes=64, name="v_first%d" % i) for i in range(2)]
         v_two = [consts.tile([P, H, HD], U32, align_bytes=64, name="v_two%d" % i) for i in range(2)]
 
         def lay_zeros():
             for h in range(H):
                 low = QUADRANT[h][TILES - 1] * 2 * Q_PARTS
-                nc.vector.memset(e_rows_three[h][:, 0, :, low : low + 2 * Q_PARTS], 0.0)
+                nc.vector.memset(e_rows_three[h][:, :, low : low + 2 * Q_PARTS], 0.0)
             for codes in v_first + v_two:
                 nc.vector.memset(codes[:].bitcast(I32), 0)
 
-        def turn_words(words, pool, name):
-            tiles = words.shape[1]
-            turned = pool.tile([P, tiles, 2, P], F32, name=name)
-            for t in range(tiles):
-                for u in range(2):
-                    nc.tensor.transpose(turned[:, t, u, :], words[:, t, u, :], ident_f32[:])
-            return turned
+        def turn_words(turned, words):
+            for u in range(2):
+                nc.tensor.transpose(turned[:, u, :], words[:, u, :], ident_f32[:])
 
         def group_words(turned, grouped):
             nc.scalar.copy(out=grouped.bitcast(F32), in_=turned[:].rearrange("p t u r -> p t r u"))
@@ -182,35 +196,30 @@ def tile_alibiattention_pa_t_kernel(tc, q, k, v, w_out, b_out, out):
 
         qk_products, turned_q, turned_k = {}, {}, {}
 
-        def turn_qk(n, which):
-            if not 0 <= n < UNITS:
-                return
-            qk_products[n, which] = pools["psum_products"].tile([P, H, P], BF16, name="product")
-            for h in range(H):
-                nc.tensor.matmul(
-                    qk_products[n, which][:, h, :],
-                    lhsT=rows_qk[n][:, which, h, :],
-                    rhs=ident_bf16[:],
-                    start=True,
-                    stop=True,
-                )
+        def turn_qk(n):
+            qk_products[n] = pools["psum_products"].tile([P, 2, H, P], BF16, name="product")
+            for which in range(2):
+                for h in range(H):
+                    nc.tensor.matmul(
+                        qk_products[n][:, which, h, :],
+                        lhsT=rows_qk[n][:, which, h, :],
+                        rhs=ident_bf16[:],
+                        start=True,
+                        stop=True,
+                    )
 
-        def copy_qk(n, which):
-            if not 0 <= n < UNITS:
-                return
+        def copy_qk(n):
             b, t = divmod(n, TILES)
-            words = qk_products[n, which][:].rearrange("d h r -> d (h r)").bitcast(F32)
-            if which == 0:
-                turned_q[n] = pools["turned_q"].tile([P, H, P], BF16, name="q_t")
-                nc.scalar.copy(out=turned_q[n][:].rearrange("d h r -> d (h r)").bitcast(F32), in_=words)
-                return
+            words = qk_products[n][:].rearrange("d w h r -> d w (h r)").bitcast(F32)
+            turned_q[n] = pools["turned_q"].tile([P, H, P], BF16, name="q_t")
+            nc.scalar.copy(out=turned_q[n][:].rearrange("d h r -> d (h r)").bitcast(F32), in_=words[:, 0, :])
             if t == 0:
                 turned_k[b] = pools["turned_k"].tile([P, H * TILES, P], BF16, name="k_t")
             for h in range(0, H, 2):
                 place = [TILES * head + QUADRANT[head][t] for head in (h, h + 1)]
                 nc.scalar.copy(
                     out=turned_k[b][:, place[0] : place[1] + 1 : place[1] - place[0], :].bitcast(F32),
-                    in_=words[:, h * P // 2 : (h + 2) * P // 2].rearrange("d (h w) -> d h w", h=2),
+                    in_=words[:, 1, h * P // 2 : (h + 2) * P // 2].rearrange("d (h w) -> d h w", h=2),
                 )
 
         jobs = [(n, i) for n in range(UNITS) for i in range(SETS[n % TILES])]
@@ -274,7 +283,14 @@ def tile_alibiattention_pa_t_kernel(tc, q, k, v, w_out, b_out, out):
             if not 0 <= j < JOBS:
                 return
             exp_biases[j] = pools["maxima"].tile([P, len(job_heads(j)[2])], F32, name="exp_bias")
-            nc.scalar.mul(exp_biases[j][:], neg_maxima[j][:], 1.0 / ROOT)
+            nc.gpsimd.tensor_scalar(
+                out=exp_biases[j][:],
+                in0=neg_maxima[j][:],
+                scalar1=1.0 / ROOT,
+                scalar2=0.0,
+                op0=ALU.mult,
+                op1=ALU.add,
+            )
 
         def soften(j):
             if not 0 <= j < JOBS:
@@ -286,11 +302,11 @@ def tile_alibiattention_pa_t_kernel(tc, q, k, v, w_out, b_out, out):
             if t == 2:
                 e_rows[j] = e_rows_three[heads[0]]
             else:
-                e_rows[j] = pools["e_rows"].tile([P, 1, 2, HALF], BF16, name="e_rows")
+                e_rows[j] = pools["e_rows"].tile([P, 2, HALF], BF16, name="e_rows")
             for i, h in enumerate(heads):
                 low = first_quadrant(h, t) * 2 * Q_PARTS
                 nc.scalar.activation(
-                    out=e_rows[j][:, 0, :, low : low + keys // 2].rearrange("r u (p x) -> r u p x", x=2),
+                    out=e_rows[j][:, :, low : low + keys // 2].rearrange("r u (p x) -> r u p x", x=2),
                     in_=scores[j][:, i * keys : (i + 1) * keys].rearrange(
                         "r (p u x) -> r u p x", u=2, x=2
                     ),
@@ -300,21 +316,25 @@ def tile_alibiattention_pa_t_kernel(tc, q, k, v, w_out, b_out, out):
                     accum_out=row_sums[n][:, h : h + 1],
                 )
 
-        def turn_e(j):
-            if not 0 <= j < JOBS:
+        def turn_e(p):
+            if not 0 <= p < PAIRS:
                 return
-            turned_e[j] = turn_words(e_rows[j][:].bitcast(F32), pools["psum_words"], "turned_e")
+            turned_e[p] = pools["psum_words"].tile([P, 2, 2, P], F32, name="turned_e")
+            for i in range(2):
+                turn_words(turned_e[p][:, i], e_rows[2 * p + i][:].bitcast(F32))
 
-        def copy_e(j):
-            if not 0 <= j < JOBS:
+        def copy_e(p):
+            if not 0 <= p < PAIRS:
                 return
-            grouped_e[j] = pools["stage"].tile([P, 1, P, PACK], BF16, align_bytes=64, name="grouped_e")
-            group_words(turned_e[j], grouped_e[j][:])
+            grouped_e[p] = pools["stage"].tile([P, 2, P, PACK], BF16, align_bytes=64, name="grouped_e")
+            group_words(turned_e[p], grouped_e[p][:])
 
-        def quantise_e(j):
-            if not 0 <= j < JOBS:
+        def quantise_e(p):
+            if not 0 <= p < PAIRS:
                 return
-            mx_e[j] = quantise(grouped_e[j][:].rearrange("p t r c -> p (t r) c"), pools["mx_e"])
+            codes, scales = quantise(grouped_e[p][:].rearrange("p t r c -> p (t r) c"), pools["mx_e"])
+            for i in range(2):
+                mx_e[2 * p + i] = (codes[:, i * P : (i + 1) * P], scales[:, i * P : (i + 1) * P])
 
         grouped_v, mx_v = {}, {}
 
@@ -373,8 +393,8 @@ def tile_alibiattention_pa_t_kernel(tc, q, k, v, w_out, b_out, out):
                 v_cols = slice(i * width, (i + 1) * width)
                 nc.tensor.matmul_mx(
                     out=o_sums[:, v_cols],
-                    lhsT=e_codes[:].bitcast(FP8X4),
-                    lhsT_scale=e_scales[:],
+                    lhsT=e_codes.bitcast(FP8X4),
+                    lhsT_scale=e_scales,
                     rhs=v_codes[:, v_cols].bitcast(FP8X4),
                     rhs_scale=v_scales[:, v_cols],
                     start=True,
@@ -391,10 +411,10 @@ def tile_alibiattention_pa_t_kernel(tc, q, k, v, w_out, b_out, out):
         def normalise(n):
             if not 0 <= n < UNITS:
                 return
-            a_rows[n] = pools["a_rows"].tile([P, 1, 2, HALF], BF16, name="a_rows")
+            a_rows[n] = pools["a_rows"].tile([P, 2, HALF], BF16, name="a_rows")
             for u in range(2):
                 nc.vector.tensor_tensor(
-                    out=a_rows[n][:, 0, u, :].rearrange("r (h p x) -> r h p x", h=H, x=2),
+                    out=a_rows[n][:, u, :].rearrange("r (h p x) -> r h p x", h=H, x=2),
                     in0=heads_sums[n][:].rearrange("r (h p u x) -> r u h p x", h=H, u=2, x=2)[:, u],
                     in1=inverse_sums[n][:].unsqueeze(2).unsqueeze(3).to_broadcast([P, H, HD // PACK, 2]),
                     op=ALU.mult,
@@ -403,7 +423,8 @@ def tile_alibiattention_pa_t_kernel(tc, q, k, v, w_out, b_out, out):
         def turn_a(n):
             if not 0 <= n < UNITS:
                 return
-            turned_a[n] = turn_words(a_rows[n][:].bitcast(F32), pools["psum_words"], "turned_e")
+            turned_a[n] = pools["psum_products"].tile([P, 1, 2, P], F32, name="product")
+            turn_words(turned_a[n][:, 0], a_rows[n][:].bitcast(F32))
 
         def copy_a(n):
             if not 0 <= n < UNITS:
@@ -444,68 +465,83 @@ def tile_alibiattention_pa_t_kernel(tc, q, k, v, w_out, b_out, out):
         grouped_w = consts.tile([P, TILES, P, PACK], BF16, align_bytes=64)
         w_codes, w_scales = [], []
 
-        products = {product_round(n): n for n in range(UNITS + LATER)}
-        turns = {}
-        for n in range(UNITS):
-            for which in range(2):
-                turns[turn_round(n, which)] = (n, which)
-        for r in range(min(turns), JOBS + 18):
-            seq, step = divmod(r, SEQ_JOBS)
-            lay_mask(r + 3)
-            turn_e(r - 1)
-            if r - 2 in products:
-                turn_a(products[r - 2])
-            if r in (1, 3):
-                turned_w[r] = turn_words(w_words[:, r - 1 : r + 1], pools["psum_products"], "product")
-            add_scores(r + 3)
-            if r in products:
-                e_times_v(products[r])
-                project(products[r] - LATER)
-            if r in turns:
-                turn_qk(*turns[r])
+        def turn_w(first):
+            turned_w[first] = pools["psum_products"].tile([P, 2, 2, P], F32, name="product")
+            for i in range(2):
+                turn_words(turned_w[first][:, i], w_words[:, first + i])
 
-            row_max(r + 2)
-            quantise_e(r - 3)
-            if r - 4 in products:
-                quantise_a(products[r - 4])
-            if r - 1 in products:
-                normalise(products[r - 1])
-                add_bias(products[r - 1] - LATER)
-            for n in range(UNITS):
-                if last_job(n) == r - 1:
-                    invert(n)
-            if r == -2:
-                lay_zeros()
-            if r == 5:
+        product_at = {r: n for n, r in enumerate(product_rounds())}
+        turn_at = {r: n for n, r in enumerate(turn_rounds())}
+        quantise_at = {r: [p for p in range(PAIRS) if quantise_round(p) == r] for r in range(PAIRS + PRODUCT_LAG)}
+
+        def quantise_left(r):
+            for p in quantise_at.get(r, ()):
+                quantise_e(p)
+            if r - LATER in product_at:
+                quantise_a(product_at[r - LATER])
+
+        for r in range(min(turn_at), max(product_at) + LATER + 2):
+            jobs_now = (2 * r, 2 * r + 1)
+            for j in jobs_now:
+                row_max(j)
+                scale_max(j)
+            if r >= PAIRS:
+                quantise_left(r)
+            if r - 1 in product_at:
+                normalise(product_at[r - 1])
+            if r - 1 - LATER in product_at:
+                add_bias(product_at[r - 1 - LATER])
+            if r < PAIRS:
+                quantise_left(r)
+            if r == 4:
                 codes, scales = quantise(grouped_w[:].rearrange("p t r c -> p (t r) c"), consts)
                 w_codes.append(codes)
                 w_scales.append(scales)
-            if r == 4:
-                quantise_v(0)
-                move_v_first(0)
-                move_v_two(0)
-            if r > 0 and step == 9:
-                quantise_v(seq + 1)
-            if r > SEQ_JOBS and step == 1:
-                move_v_two(seq)
-            if r > SEQ_JOBS and step == 4:
-                move_v_first(seq)
-            if 0 <= r < 4:
-                group_v(0, r)
-            if r >= 0 and step % 2 == 0 and step < 2 * H:
-                group_v(seq + 1, step // 2)
+            for b in range(B):
+                if r == v_round(b):
+                    quantise_v(b)
 
-            scale_max(r + 1)
-            soften(r)
-            copy_e(r - 2)
-            if r - 1 in turns:
-                copy_qk(*turns[r - 1])
-            if r - 3 in products:
-                copy_a(products[r - 3])
-            if r in (2, 4):
-                group_words(turned_w[r - 1], grouped_w[:, r - 2 : r])
+            for j in jobs_now:
+                lay_mask(j + 2)
+            turn_e(r - 1)
+            if r - 2 in product_at:
+                turn_a(product_at[r - 2])
+            if r in (2, 3):
+                turn_w(2 * (r - 2))
+            for j in jobs_now:
+                add_scores(j + 2)
+            if r in turn_at:
+                turn_qk(turn_at[r])
+            if r in product_at:
+                e_times_v(product_at[r])
+            if r - LATER in product_at:
+                project(product_at[r - LATER])
 
-            if r in turns and turns[r][1] == 0:
-                load_qk(turns[r][0] + LOADS_AHEAD)
-            if r >= 0 and step == 2:
-                load_v(seq + 2)
+            for n in range(UNITS):
+                if last_job(n) // 2 == r - 1:
+                    invert(n)
+            if r == -1:
+                lay_zeros()
+            for b in range(B):
+                for h in range(H):
+                    if r == max(v_round(b) - H + h, 0):
+                        group_v(b, h)
+                if r == v_round(b):
+                    move_v_first(b)
+                    move_v_two(b)
+
+            if r - 1 in turn_at:
+                copy_qk(turn_at[r - 1])
+            for j in jobs_now:
+                soften(j)
+            copy_e(r - 1)
+            if r - 2 in product_at:
+                copy_a(product_at[r - 2])
+            if r in (2, 3):
+                group_words(turned_w[2 * (r - 2)], grouped_w[:, 2 * (r - 2) : 2 * (r - 1)])
+
+            if r in turn_at:
+                load_qk(turn_at[r] + LOADS_AHEAD)
+            for b in range(B):
+                if r == v_round(b) - 1:
+                    load_v(b + 1)

@@ -30,9 +30,11 @@ SETS = (1, 2, 4, 4)
 SEQ_JOBS = sum(SETS)
 JOBS = B * SEQ_JOBS
 PAIRS = JOBS // 2
-PSUM_RINGS = (("psum_scores", 4), ("psum_words", 1), ("psum_products", 3))
-PRODUCT_LAG = 3
-LATER = 3
+PSUM_BANKS = 8
+QUANTISE_LAG = 3
+PRODUCT_LAG = 4
+A_LAG = 3
+PROJECT_LAG = 4
 TURN_LEAD = 3
 LOADS_AHEAD = 4
 
@@ -52,14 +54,10 @@ def v_round(b):
     return last_job(TILES * b) // 2 + 2
 
 
-def quantise_round(p):
-    return p + PRODUCT_LAG - (p >= PAIRS - 2)
-
-
 def product_rounds():
     rounds = []
     for n in range(UNITS):
-        earliest = quantise_round(last_job(n) // 2)
+        earliest = last_job(n) // 2 + PRODUCT_LAG
         rounds.append(max(earliest, rounds[-1] + 1) if rounds else earliest)
     return rounds
 
@@ -83,22 +81,20 @@ def tile_alibiattention_pa_t_kernel(tc, q, k, v, w_out, b_out, out):
                 ("consts", 1),
                 ("rows_qk", 6),
                 ("rows_v", 3),
-                ("turned_q", 5),
-                ("turned_k", 3),
-                ("maxima", 4),
+                ("turned_qk", 8),
+                ("maxima", 6),
                 ("sums", 8),
                 ("e_rows", 4),
                 ("stage", 3),
                 ("stage_v", 2),
-                ("mx_e", 8),
+                ("mx_e", 10),
                 ("mx_v", 2),
                 ("a_rows", 3),
                 ("mx_a", 5),
                 ("result", 4),
             )
         }
-        for name, bufs in PSUM_RINGS:
-            pools[name] = stack.enter_context(tc.psum_pool(name=name, bufs=bufs))
+        pools["psum"] = stack.enter_context(tc.psum_pool(name="psum", bufs=PSUM_BANKS))
         consts = pools["consts"]
 
         rows_qk, rows_v = {}, {}
@@ -194,10 +190,10 @@ def tile_alibiattention_pa_t_kernel(tc, q, k, v, w_out, b_out, out):
             )
             return codes, scales
 
-        qk_products, turned_q, turned_k = {}, {}, {}
+        qk_products, turned_qk = {}, {}
 
         def turn_qk(n):
-            qk_products[n] = pools["psum_products"].tile([P, 2, H, P], BF16, name="product")
+            qk_products[n] = pools["psum"].tile([P, 2, H, P], BF16, name="bank")
             for which in range(2):
                 for h in range(H):
                     nc.tensor.matmul(
@@ -209,18 +205,11 @@ def tile_alibiattention_pa_t_kernel(tc, q, k, v, w_out, b_out, out):
                     )
 
         def copy_qk(n):
-            b, t = divmod(n, TILES)
-            words = qk_products[n][:].rearrange("d w h r -> d w (h r)").bitcast(F32)
-            turned_q[n] = pools["turned_q"].tile([P, H, P], BF16, name="q_t")
-            nc.scalar.copy(out=turned_q[n][:].rearrange("d h r -> d (h r)").bitcast(F32), in_=words[:, 0, :])
-            if t == 0:
-                turned_k[b] = pools["turned_k"].tile([P, H * TILES, P], BF16, name="k_t")
-            for h in range(0, H, 2):
-                place = [TILES * head + QUADRANT[head][t] for head in (h, h + 1)]
-                nc.scalar.copy(
-                    out=turned_k[b][:, place[0] : place[1] + 1 : place[1] - place[0], :].bitcast(F32),
-                    in_=words[:, 1, h * P // 2 : (h + 2) * P // 2].rearrange("d (h w) -> d h w", h=2),
-                )
+            turned_qk[n] = pools["turned_qk"].tile([P, 2, H, P], BF16, name="qk_t")
+            nc.scalar.copy(
+                out=turned_qk[n][:].rearrange("d w h r -> d (w h r)").bitcast(F32),
+                in_=qk_products[n][:].rearrange("d w h r -> d (w h r)").bitcast(F32),
+            )
 
         jobs = [(n, i) for n in range(UNITS) for i in range(SETS[n % TILES])]
         scores, neg_maxima, exp_biases, row_sums, e_rows, turned_e, grouped_e, mx_e = {}, {}, {}, {}, {}, {}, {}, {}
@@ -235,7 +224,7 @@ def tile_alibiattention_pa_t_kernel(tc, q, k, v, w_out, b_out, out):
                 return
             n, t, heads = job_heads(j)
             keys = (t + 1) * P
-            scores[j] = pools["psum_scores"].tile([P, S], F32, name="s_sums")
+            scores[j] = pools["psum"].tile([P, S], F32, name="bank")
             for i, h in enumerate(heads):
                 for place in range(t + 1):
                     m = QUADRANT[h].index(first_quadrant(h, t) + place)
@@ -252,17 +241,17 @@ def tile_alibiattention_pa_t_kernel(tc, q, k, v, w_out, b_out, out):
             if not 0 <= j < JOBS:
                 return
             n, t, heads = job_heads(j)
-            keys = (t + 1) * P
-            k_t = turned_k[n // TILES][:].rearrange("d b j -> d (b j)")
             for i, h in enumerate(heads):
-                first = h * S + first_quadrant(h, t) * P
-                nc.tensor.matmul(
-                    scores[j][:, i * keys : (i + 1) * keys],
-                    lhsT=turned_q[n][:, h, :],
-                    rhs=k_t[:, first : first + keys],
-                    start=False,
-                    stop=h == heads[-1],
-                )
+                for place in range(t + 1):
+                    m = QUADRANT[h].index(first_quadrant(h, t) + place)
+                    block = i * (t + 1) + place
+                    nc.tensor.matmul(
+                        scores[j][:, block * P : (block + 1) * P],
+                        lhsT=turned_qk[n][:, 0, h, :],
+                        rhs=turned_qk[n - t + m][:, 1, h, :],
+                        start=False,
+                        stop=h == heads[-1] and place == t,
+                    )
 
         def row_max(j):
             if not 0 <= j < JOBS:
@@ -297,8 +286,10 @@ def tile_alibiattention_pa_t_kernel(tc, q, k, v, w_out, b_out, out):
                 return
             n, t, heads = job_heads(j)
             keys = (t + 1) * P
-            if heads[0] == 0:
-                row_sums[n] = pools["sums"].tile([P, H], F32, name="row_sum")
+            if heads[0] == 0 and n % 2 == 0:
+                row_sum = pools["sums"].tile([P, 2, H], F32, name="row_sum")
+                row_sums[n], row_sums[n + 1] = row_sum[:, 0, :], row_sum[:, 1, :]
+                pair_sums[n] = row_sum
             if t == 2:
                 e_rows[j] = e_rows_three[heads[0]]
             else:
@@ -319,7 +310,7 @@ def tile_alibiattention_pa_t_kernel(tc, q, k, v, w_out, b_out, out):
         def turn_e(p):
             if not 0 <= p < PAIRS:
                 return
-            turned_e[p] = pools["psum_words"].tile([P, 2, 2, P], F32, name="turned_e")
+            turned_e[p] = pools["psum"].tile([P, 2, 2, P], F32, name="bank")
             for i in range(2):
                 turn_words(turned_e[p][:, i], e_rows[2 * p + i][:].bitcast(F32))
 
@@ -338,15 +329,16 @@ def tile_alibiattention_pa_t_kernel(tc, q, k, v, w_out, b_out, out):
 
         grouped_v, mx_v = {}, {}
 
-        def group_v(b, h):
+        def group_v(b, first):
             if b >= B:
                 return
-            if h == 0:
+            if first == 0:
                 grouped_v[b] = pools["stage_v"].tile(
                     [P, H, HD, PACK], BF16, align_bytes=64, name="grouped_v"
                 )
+            heads = slice(first, first + 2)
             nc.vector.tensor_copy(
-                out=grouped_v[b][:, h, :, :], in_=rows_v[b][:, h, :, :].rearrange("p c d -> p d c")
+                out=grouped_v[b][:, heads, :, :], in_=rows_v[b][:, heads, :, :].rearrange("p h c d -> p h d c")
             )
 
         def quantise_v(b):
@@ -361,7 +353,7 @@ def tile_alibiattention_pa_t_kernel(tc, q, k, v, w_out, b_out, out):
             two = v_two[b % 2][:].bitcast(I32)
             for low in range(2):
                 part = slice(low * P // 2, (low + 1) * P // 2)
-                nc.vector.tensor_copy(out=two[part, low::2, :], in_=codes[part, low::2, :])
+                nc.sync.dma_start(out=two[part, low::2, :], in_=codes[part, low::2, :])
 
         def move_v_first(b):
             if b >= B:
@@ -371,9 +363,9 @@ def tile_alibiattention_pa_t_kernel(tc, q, k, v, w_out, b_out, out):
             for h in range(H):
                 low = QUADRANT[h][0] * Q_PARTS
                 part = slice(low, low + Q_PARTS)
-                nc.vector.tensor_copy(out=one_block[part, h, :], in_=codes[part, h, :])
+                nc.sync.dma_start(out=one_block[part, h, :], in_=codes[part, h, :])
 
-        heads_sums, inverse_sums, a_rows, turned_a, grouped_a, mx_a, out_sums = {}, {}, {}, {}, {}, {}, {}
+        pair_sums, heads_sums, inverse_sums, a_rows, turned_a, grouped_a, mx_a, out_sums = {}, {}, {}, {}, {}, {}, {}, {}
 
         def e_times_v(n):
             if not 0 <= n < UNITS:
@@ -386,7 +378,7 @@ def tile_alibiattention_pa_t_kernel(tc, q, k, v, w_out, b_out, out):
                 v_codes = v_two[b % 2][:].rearrange("p h d -> p (h d)")
             else:
                 v_codes = v_codes[:]
-            o_sums = pools["psum_products"].tile([P, D], F32, name="product")
+            o_sums = pools["psum"].tile([P, D], F32, name="bank")
             width = D // SETS[t]
             for i in range(SETS[t]):
                 e_codes, e_scales = mx_e[last_job(n) - SETS[t] + 1 + i]
@@ -403,27 +395,25 @@ def tile_alibiattention_pa_t_kernel(tc, q, k, v, w_out, b_out, out):
             heads_sums[n] = o_sums
 
         def invert(n):
-            if not 0 <= n < UNITS:
-                return
-            inverse_sums[n] = pools["sums"].tile([P, H], F32, name="one_over_sum")
-            nc.vector.reciprocal(out=inverse_sums[n][:], in_=row_sums[n][:])
+            one_over_sum = pools["sums"].tile([P, 2, H], F32)
+            nc.vector.reciprocal(out=one_over_sum[:], in_=pair_sums[n][:])
+            inverse_sums[n], inverse_sums[n + 1] = one_over_sum[:, 0, :], one_over_sum[:, 1, :]
 
         def normalise(n):
             if not 0 <= n < UNITS:
                 return
             a_rows[n] = pools["a_rows"].tile([P, 2, HALF], BF16, name="a_rows")
-            for u in range(2):
-                nc.vector.tensor_tensor(
-                    out=a_rows[n][:, u, :].rearrange("r (h p x) -> r h p x", h=H, x=2),
-                    in0=heads_sums[n][:].rearrange("r (h p u x) -> r u h p x", h=H, u=2, x=2)[:, u],
-                    in1=inverse_sums[n][:].unsqueeze(2).unsqueeze(3).to_broadcast([P, H, HD // PACK, 2]),
-                    op=ALU.mult,
-                )
+            nc.vector.tensor_tensor(
+                out=a_rows[n][:].rearrange("r u c -> r (u c)").rearrange("r (h d) -> r h d", h=H),
+                in0=heads_sums[n][:].rearrange("r (h d) -> r h d", h=H),
+                in1=inverse_sums[n].unsqueeze(2).to_broadcast([P, H, HD]),
+                op=ALU.mult,
+            )
 
         def turn_a(n):
             if not 0 <= n < UNITS:
                 return
-            turned_a[n] = pools["psum_products"].tile([P, 1, 2, P], F32, name="product")
+            turned_a[n] = pools["psum"].tile([P, 1, 2, P], F32, name="bank")
             turn_words(turned_a[n][:, 0], a_rows[n][:].bitcast(F32))
 
         def copy_a(n):
@@ -441,7 +431,7 @@ def tile_alibiattention_pa_t_kernel(tc, q, k, v, w_out, b_out, out):
             if not 0 <= n < UNITS:
                 return
             a_codes, a_scales = mx_a[n]
-            out_sums[n] = pools["psum_products"].tile([P, D], F32, name="product")
+            out_sums[n] = pools["psum"].tile([P, D], F32, name="bank")
             nc.tensor.matmul_mx(
                 out=out_sums[n][:],
                 lhsT=a_codes[:].bitcast(FP8X4),
@@ -460,83 +450,73 @@ def tile_alibiattention_pa_t_kernel(tc, q, k, v, w_out, b_out, out):
             nc.vector.tensor_tensor(out=result[:], in0=out_sums[n][:], in1=bias[:], op=ALU.add)
             nc.sync.dma_start(out=out[b, t * P : (t + 1) * P, :], in_=result[:])
 
-        w_words = w_rows[:].bitcast(F32).rearrange("r t (p u) -> r t u p", u=2)
+        w_words = w_rows[:].bitcast(F32).rearrange("r t (u p) -> r t u p", u=2)
         turned_w = {}
         grouped_w = consts.tile([P, TILES, P, PACK], BF16, align_bytes=64)
         w_codes, w_scales = [], []
 
         def turn_w(first):
-            turned_w[first] = pools["psum_products"].tile([P, 2, 2, P], F32, name="product")
+            turned_w[first] = pools["psum"].tile([P, 2, 2, P], F32, name="bank")
             for i in range(2):
                 turn_words(turned_w[first][:, i], w_words[:, first + i])
 
         product_at = {r: n for n, r in enumerate(product_rounds())}
         turn_at = {r: n for n, r in enumerate(turn_rounds())}
-        quantise_at = {r: [p for p in range(PAIRS) if quantise_round(p) == r] for r in range(PAIRS + PRODUCT_LAG)}
-
-        def quantise_left(r):
-            for p in quantise_at.get(r, ()):
-                quantise_e(p)
-            if r - LATER in product_at:
-                quantise_a(product_at[r - LATER])
-
-        for r in range(min(turn_at), max(product_at) + LATER + 2):
+        for r in range(min(turn_at), max(product_at) + PROJECT_LAG + 1):
             jobs_now = (2 * r, 2 * r + 1)
-            for j in jobs_now:
-                row_max(j)
-                scale_max(j)
-            if r >= PAIRS:
-                quantise_left(r)
-            if r - 1 in product_at:
-                normalise(product_at[r - 1])
-            if r - 1 - LATER in product_at:
-                add_bias(product_at[r - 1 - LATER])
-            if r < PAIRS:
-                quantise_left(r)
-            if r == 4:
+            quantise_e(r - QUANTISE_LAG)
+            if r - A_LAG in product_at:
+                quantise_a(product_at[r - A_LAG])
+            if r == 5:
                 codes, scales = quantise(grouped_w[:].rearrange("p t r c -> p (t r) c"), consts)
                 w_codes.append(codes)
                 w_scales.append(scales)
             for b in range(B):
                 if r == v_round(b):
                     quantise_v(b)
-
-            for j in jobs_now:
-                lay_mask(j + 2)
-            turn_e(r - 1)
-            if r - 2 in product_at:
-                turn_a(product_at[r - 2])
-            if r in (2, 3):
-                turn_w(2 * (r - 2))
-            for j in jobs_now:
-                add_scores(j + 2)
-            if r in turn_at:
-                turn_qk(turn_at[r])
-            if r in product_at:
-                e_times_v(product_at[r])
-            if r - LATER in product_at:
-                project(product_at[r - LATER])
-
-            for n in range(UNITS):
-                if last_job(n) // 2 == r - 1:
-                    invert(n)
-            if r == -1:
-                lay_zeros()
-            for b in range(B):
-                for h in range(H):
-                    if r == max(v_round(b) - H + h, 0):
-                        group_v(b, h)
-                if r == v_round(b):
                     move_v_first(b)
                     move_v_two(b)
 
-            if r - 1 in turn_at:
-                copy_qk(turn_at[r - 1])
+            if r in product_at:
+                e_times_v(product_at[r])
+            if r - PROJECT_LAG in product_at:
+                project(product_at[r - PROJECT_LAG])
+            if r in turn_at:
+                turn_qk(turn_at[r])
+            turn_e(r - 1)
+            if r - 1 in product_at:
+                turn_a(product_at[r - 1])
+            if r in (2, 3):
+                turn_w(2 * (r - 2))
             for j in jobs_now:
-                soften(j)
-            copy_e(r - 1)
+                lay_mask(j + 2)
+            for j in jobs_now:
+                add_scores(j + 2)
+
+            for j in jobs_now:
+                row_max(j)
+                scale_max(j)
+            for n in range(0, UNITS, 2):
+                if last_job(n + 1) // 2 == r - 1:
+                    invert(n)
+            if r in product_at:
+                normalise(product_at[r])
+            if r - PROJECT_LAG in product_at:
+                add_bias(product_at[r - PROJECT_LAG])
+            if r == -1:
+                lay_zeros()
+            for b in range(B):
+                for first in (0, 2):
+                    if r == max(v_round(b) - 2 + first // 2, 0):
+                        group_v(b, first)
+
+            copy_e(r - 2)
             if r - 2 in product_at:
                 copy_a(product_at[r - 2])
+            soften(2 * r)
+            if r in turn_at:
+                copy_qk(turn_at[r])
+            soften(2 * r + 1)
             if r in (2, 3):
                 group_words(turned_w[2 * (r - 2)], grouped_w[:, 2 * (r - 2) : 2 * (r - 1)])
 

@@ -30,12 +30,16 @@ SETS = (1, 2, 4, 4)
 SEQ_JOBS = sum(SETS)
 JOBS = B * SEQ_JOBS
 PAIRS = JOBS // 2
+TWO_SEQ_PAIRS = SEQ_JOBS
+V_STEPS = ((-5, -3, -1), (1, 2, 6))
+V_LOAD_LEAD = 4
 PSUM_BANKS = 8
 QUANTISE_LAG = 3
 PRODUCT_LAG = 4
 A_LAG = 3
 PROJECT_LAG = 4
 TURN_LEAD = 3
+WARM_UP = 9
 LOADS_AHEAD = 4
 
 FLOPS = 2 * (2 * B * H * S * S * HD) + 2 * B * S * D * D
@@ -50,8 +54,12 @@ def last_job(n):
     return SEQ_JOBS * b + sum(SETS[: t + 1]) - 1
 
 
-def v_round(b):
-    return last_job(TILES * b) // 2 + 2
+def on_scalar(n):
+    return n % TILES == 3
+
+
+def v_rounds(b):
+    return ((1, 2, 3), (3, 4, 6))[b] if b < 2 else tuple(TWO_SEQ_PAIRS * (b // 2) + step for step in V_STEPS[b % 2])
 
 
 def product_rounds():
@@ -66,8 +74,8 @@ def turn_rounds():
     rounds = []
     for n in reversed(range(UNITS)):
         first_job = last_job(n) - SETS[n % TILES] + 1
-        latest = first_job // 2 - TURN_LEAD
-        rounds.append(min(latest, rounds[-1] - 1) if rounds else latest)
+        r = min([first_job // 2 - TURN_LEAD] + [later - 1 for later in rounds[-1:]])
+        rounds.append(r - (r > 0 and r % TWO_SEQ_PAIRS == 0))
     return rounds[::-1]
 
 
@@ -79,7 +87,7 @@ def tile_alibiattention_pa_t_kernel(tc, q, k, v, w_out, b_out, out):
             name: stack.enter_context(tc.tile_pool(name=name, bufs=bufs))
             for name, bufs in (
                 ("consts", 1),
-                ("rows_qk", 6),
+                ("rows_qk", 7),
                 ("rows_v", 3),
                 ("turned_qk", 8),
                 ("maxima", 6),
@@ -129,34 +137,46 @@ def tile_alibiattention_pa_t_kernel(tc, q, k, v, w_out, b_out, out):
                     m = after
             rows_v[b] = rows
 
-        for n in range(LOADS_AHEAD - 1):
+        for n in range(LOADS_AHEAD):
             load_qk(n)
         load_v(0)
+        load_qk(LOADS_AHEAD)
         w_rows = consts.tile([P, TILES, D], BF16)
         nc.sync.dma_start(out=w_rows[:], in_=w_out.rearrange("(t r) c -> r t c", r=P))
-        load_qk(LOADS_AHEAD - 1)
+        load_qk(LOADS_AHEAD + 1)
+        load_qk(LOADS_AHEAD + 2)
         bias = consts.tile([P, D], BF16)
         nc.sync.dma_start(out=bias[:], in_=b_out.partition_broadcast(P))
+        load_v(1)
 
+        distance = consts.tile([P, TILES, P], I32)
+        alibi = consts.tile([P, TILES, P], F32)
+        ident_f32 = consts.tile([P, P], F32)
         ident_bf16 = consts.tile([P, P], BF16)
         make_identity(nc, ident_bf16[:])
-        distance = consts.tile([P, TILES, P], I32)
-        nc.gpsimd.iota(distance[:], pattern=[[-P, TILES], [-1, P]], base=0, channel_multiplier=1)
-        ident_f32 = consts.tile([P, P], F32)
+        nc.gpsimd.iota(distance[:, 0, :], pattern=[[-1, P]], base=0, channel_multiplier=1)
         make_identity(nc, ident_f32[:])
-        alibi = consts.tile([P, TILES, P], F32)
-        nc.vector.tensor_copy(out=alibi[:], in_=distance[:])
-        nc.vector.tensor_scalar(out=alibi[:], in0=alibi[:], scalar1=ROOT, scalar2=None, op0=ALU.mult)
+        nc.gpsimd.iota(distance[:, 1:, :], pattern=[[-P, TILES - 1], [-1, P]], base=-P, channel_multiplier=1)
         future = consts.tile([P, P], F32)
         nc.vector.tensor_scalar(
             out=future[:],
-            in0=alibi[:, 0, :],
+            in0=distance[:, 0, :],
             scalar1=0.0,
             scalar2=ROOT * NEG_INF,
             op0=ALU.is_gt,
             op1=ALU.mult,
         )
-        nc.vector.tensor_tensor(out=alibi[:, 0, :], in0=alibi[:, 0, :], in1=future[:], op=ALU.add)
+        nc.vector.scalar_tensor_tensor(
+            out=alibi[:, 0, :],
+            in0=distance[:, 0, :],
+            scalar=ROOT,
+            in1=future[:],
+            op0=ALU.mult,
+            op1=ALU.add,
+        )
+        nc.vector.tensor_scalar(
+            out=alibi[:, 1:, :], in0=distance[:, 1:, :], scalar1=ROOT, scalar2=None, op0=ALU.mult
+        )
 
         zero = consts.tile([P, 1], F32)
         nc.vector.memset(zero[:], 0.0)
@@ -167,11 +187,13 @@ def tile_alibiattention_pa_t_kernel(tc, q, k, v, w_out, b_out, out):
         v_first = [consts.tile([P, H, HD], U32, align_bytes=64, name="v_first%d" % i) for i in range(2)]
         v_two = [consts.tile([P, H, HD], U32, align_bytes=64, name="v_two%d" % i) for i in range(2)]
 
-        def lay_zeros():
+        def lay_zeros_e():
             for h in range(H):
                 low = QUADRANT[h][TILES - 1] * 2 * Q_PARTS
                 nc.vector.memset(e_rows_three[h][:, :, low : low + 2 * Q_PARTS], 0.0)
-            for codes in v_first + v_two:
+
+        def lay_zeros_v(b):
+            for codes in (v_first[b % 2], v_two[b % 2]):
                 nc.vector.memset(codes[:].bitcast(I32), 0)
 
         def turn_words(turned, words):
@@ -351,19 +373,21 @@ def tile_alibiattention_pa_t_kernel(tc, q, k, v, w_out, b_out, out):
                 return
             codes = mx_v[b][0][:].rearrange("p (h d) -> p h d", h=H).bitcast(I32)
             two = v_two[b % 2][:].bitcast(I32)
+            move = nc.sync.dma_start if b > 0 else nc.vector.tensor_copy
             for low in range(2):
                 part = slice(low * P // 2, (low + 1) * P // 2)
-                nc.sync.dma_start(out=two[part, low::2, :], in_=codes[part, low::2, :])
+                move(out=two[part, low::2, :], in_=codes[part, low::2, :])
 
         def move_v_first(b):
             if b >= B:
                 return
             codes = mx_v[b][0][:].rearrange("p (h d) -> p h d", h=H).bitcast(I32)
             one_block = v_first[b % 2][:].bitcast(I32)
+            move = nc.sync.dma_start if b > 0 else nc.vector.tensor_copy
             for h in range(H):
                 low = QUADRANT[h][0] * Q_PARTS
                 part = slice(low, low + Q_PARTS)
-                nc.sync.dma_start(out=one_block[part, h, :], in_=codes[part, h, :])
+                move(out=one_block[part, h, :], in_=codes[part, h, :])
 
         pair_sums, heads_sums, inverse_sums, a_rows, turned_a, grouped_a, mx_a, out_sums = {}, {}, {}, {}, {}, {}, {}, {}
 
@@ -403,6 +427,15 @@ def tile_alibiattention_pa_t_kernel(tc, q, k, v, w_out, b_out, out):
             if not 0 <= n < UNITS:
                 return
             a_rows[n] = pools["a_rows"].tile([P, 2, HALF], BF16, name="a_rows")
+            if on_scalar(n):
+                for h in range(H):
+                    nc.scalar.activation(
+                        out=a_rows[n][:].rearrange("r u c -> r (u c)")[:, h * HD : (h + 1) * HD],
+                        in_=heads_sums[n][:, h * HD : (h + 1) * HD],
+                        func=FUNC.Copy,
+                        scale=inverse_sums[n][:, h : h + 1],
+                    )
+                return
             nc.vector.tensor_tensor(
                 out=a_rows[n][:].rearrange("r u c -> r (u c)").rearrange("r (h d) -> r h d", h=H),
                 in0=heads_sums[n][:].rearrange("r (h d) -> r h d", h=H),
@@ -462,7 +495,28 @@ def tile_alibiattention_pa_t_kernel(tc, q, k, v, w_out, b_out, out):
 
         product_at = {r: n for n, r in enumerate(product_rounds())}
         turn_at = {r: n for n, r in enumerate(turn_rounds())}
-        for r in range(min(turn_at), max(product_at) + PROJECT_LAG + 1):
+        warm = pools["psum"].tile([P, TILES, P], F32, name="bank")
+        for i in range(WARM_UP):
+            nc.tensor.matmul(warm[:, i % TILES, :], lhsT=ident_bf16[:], rhs=ident_bf16[:], start=True, stop=True)
+        first_units = [n for r, n in sorted(turn_at.items()) if r < 0]
+        lay_mask(0)
+        lay_mask(1)
+        for n in first_units[:2]:
+            turn_qk(n)
+            copy_qk(n)
+        add_scores(0)
+        add_scores(1)
+        for n in first_units[2:]:
+            turn_qk(n)
+        lay_zeros_e()
+        lay_zeros_v(0)
+        lay_zeros_v(1)
+        row_max(0)
+        scale_max(0)
+        soften(0)
+        for n in first_units[2:]:
+            copy_qk(n)
+        for r in range(PAIRS):
             jobs_now = (2 * r, 2 * r + 1)
             quantise_e(r - QUANTISE_LAG)
             if r - A_LAG in product_at:
@@ -472,7 +526,7 @@ def tile_alibiattention_pa_t_kernel(tc, q, k, v, w_out, b_out, out):
                 w_codes.append(codes)
                 w_scales.append(scales)
             for b in range(B):
-                if r == v_round(b):
+                if r == v_rounds(b)[2]:
                     quantise_v(b)
                     move_v_first(b)
                     move_v_two(b)
@@ -494,34 +548,56 @@ def tile_alibiattention_pa_t_kernel(tc, q, k, v, w_out, b_out, out):
                 add_scores(j + 2)
 
             for j in jobs_now:
-                row_max(j)
-                scale_max(j)
+                if j > 0:
+                    row_max(j)
+                    scale_max(j)
             for n in range(0, UNITS, 2):
                 if last_job(n + 1) // 2 == r - 1:
                     invert(n)
-            if r in product_at:
+            if r in product_at and not on_scalar(product_at[r]):
                 normalise(product_at[r])
             if r - PROJECT_LAG in product_at:
                 add_bias(product_at[r - PROJECT_LAG])
-            if r == -1:
-                lay_zeros()
             for b in range(B):
                 for first in (0, 2):
-                    if r == max(v_round(b) - 2 + first // 2, 0):
+                    if r == v_rounds(b)[first // 2]:
                         group_v(b, first)
 
             copy_e(r - 2)
             if r - 2 in product_at:
                 copy_a(product_at[r - 2])
-            soften(2 * r)
+            if r > 0:
+                soften(2 * r)
             if r in turn_at:
                 copy_qk(turn_at[r])
             soften(2 * r + 1)
+            if r in product_at and on_scalar(product_at[r]):
+                normalise(product_at[r])
             if r in (2, 3):
                 group_words(turned_w[2 * (r - 2)], grouped_w[:, 2 * (r - 2) : 2 * (r - 1)])
 
             if r in turn_at:
                 load_qk(turn_at[r] + LOADS_AHEAD)
             for b in range(B):
-                if r == v_round(b) - 1:
-                    load_v(b + 1)
+                if r == v_rounds(b)[0] - V_LOAD_LEAD and b > 1:
+                    load_v(b)
+
+        stages = (e_times_v, normalise, turn_a, copy_a, quantise_a, project, add_bias)
+        rounds_after = (0, 0, 1, 2, 3, 4, 4)
+        left = {n: sum(r + after < PAIRS for after in rounds_after) for r, n in product_at.items()}
+        copy_e(PAIRS - 2)
+        turn_e(PAIRS - 1)
+        copy_e(PAIRS - 1)
+        for p in range(PAIRS - QUANTISE_LAG, PAIRS):
+            quantise_e(p)
+            if p == PAIRS - QUANTISE_LAG:
+                invert(UNITS - 2)
+            for n in sorted(left, reverse=True):
+                if last_job(n) // 2 <= p and left[n] < len(stages):
+                    stages[left[n]](n)
+                    left[n] += 1
+        while min(left.values()) < len(stages):
+            for n in sorted(left, reverse=True):
+                if left[n] < len(stages):
+                    stages[left[n]](n)
+                    left[n] += 1

@@ -35,7 +35,7 @@ V_STEPS = ((-5, -3, -1), (1, 2, 6))
 V_LOAD_LEAD = 4
 PSUM_BANKS = 8
 QUANTISE_LAG = 3
-PRODUCT_LAG = 4
+PRODUCT_LAG = 3
 A_LAG = 3
 PROJECT_LAG = 4
 TURN_LEAD = 3
@@ -65,7 +65,7 @@ def v_rounds(b):
 def product_rounds():
     rounds = []
     for n in range(UNITS):
-        earliest = last_job(n) // 2 + PRODUCT_LAG
+        earliest = last_job(n) // 4 * 2 + 1 + PRODUCT_LAG
         rounds.append(max(earliest, rounds[-1] + 1) if rounds else earliest)
     return rounds
 
@@ -93,9 +93,10 @@ def tile_alibiattention_pa_t_kernel(tc, q, k, v, w_out, b_out, out):
                 ("maxima", 6),
                 ("sums", 8),
                 ("e_rows", 4),
+                ("stage_e", 3),
                 ("stage", 3),
                 ("stage_v", 2),
-                ("mx_e", 10),
+                ("mx_e", 5),
                 ("mx_v", 2),
                 ("a_rows", 3),
                 ("mx_a", 5),
@@ -339,15 +340,17 @@ def tile_alibiattention_pa_t_kernel(tc, q, k, v, w_out, b_out, out):
         def copy_e(p):
             if not 0 <= p < PAIRS:
                 return
-            grouped_e[p] = pools["stage"].tile([P, 2, P, PACK], BF16, align_bytes=64, name="grouped_e")
-            group_words(turned_e[p], grouped_e[p][:])
+            if p % 2 == 0:
+                grouped_e[p // 2] = pools["stage_e"].tile([P, 4, P, PACK], BF16, align_bytes=64, name="grouped_e")
+            half = slice(p % 2 * 2, p % 2 * 2 + 2)
+            group_words(turned_e[p], grouped_e[p // 2][:, half])
 
         def quantise_e(p):
-            if not 0 <= p < PAIRS:
+            if not 0 <= p < PAIRS or p % 2 == 0:
                 return
-            codes, scales = quantise(grouped_e[p][:].rearrange("p t r c -> p (t r) c"), pools["mx_e"])
-            for i in range(2):
-                mx_e[2 * p + i] = (codes[:, i * P : (i + 1) * P], scales[:, i * P : (i + 1) * P])
+            codes, scales = quantise(grouped_e[p // 2][:].rearrange("p t r c -> p (t r) c"), pools["mx_e"])
+            for i in range(4):
+                mx_e[2 * p - 2 + i] = (codes[:, i * P : (i + 1) * P], scales[:, i * P : (i + 1) * P])
 
         grouped_v, mx_v = {}, {}
 
@@ -360,7 +363,8 @@ def tile_alibiattention_pa_t_kernel(tc, q, k, v, w_out, b_out, out):
                 )
             heads = slice(first, first + 2)
             nc.vector.tensor_copy(
-                out=grouped_v[b][:, heads, :, :], in_=rows_v[b][:, heads, :, :].rearrange("p h c d -> p h d c")
+                out=grouped_v[b][:, heads, :, :].rearrange("p h (d i) c -> p h d c i", i=PACK),
+                in_=rows_v[b][:, heads, :, :].rearrange("p h c (d i) -> p h d c i", i=PACK),
             )
 
         def quantise_v(b):
@@ -537,15 +541,14 @@ def tile_alibiattention_pa_t_kernel(tc, q, k, v, w_out, b_out, out):
                 project(product_at[r - PROJECT_LAG])
             if r in turn_at:
                 turn_qk(turn_at[r])
-            turn_e(r - 1)
-            if r - 1 in product_at:
-                turn_a(product_at[r - 1])
             if r in (2, 3):
                 turn_w(2 * (r - 2))
             for j in jobs_now:
                 lay_mask(j + 2)
-            for j in jobs_now:
                 add_scores(j + 2)
+            turn_e(r - 1)
+            if r - 1 in product_at:
+                turn_a(product_at[r - 1])
 
             for j in jobs_now:
                 if j > 0:
@@ -590,14 +593,9 @@ def tile_alibiattention_pa_t_kernel(tc, q, k, v, w_out, b_out, out):
         copy_e(PAIRS - 1)
         for p in range(PAIRS - QUANTISE_LAG, PAIRS):
             quantise_e(p)
-            if p == PAIRS - QUANTISE_LAG:
-                invert(UNITS - 2)
-            for n in sorted(left, reverse=True):
-                if last_job(n) // 2 <= p and left[n] < len(stages):
-                    stages[left[n]](n)
-                    left[n] += 1
+        invert(UNITS - 2)
         while min(left.values()) < len(stages):
-            for n in sorted(left, reverse=True):
+            for n in sorted(left):
                 if left[n] < len(stages):
                     stages[left[n]](n)
                     left[n] += 1

@@ -36,8 +36,8 @@ V_LOAD_LEAD = 4
 PSUM_BANKS = 8
 QUANTISE_LAG = 3
 PRODUCT_LAG = 3
-A_LAG = 3
-PROJECT_LAG = 4
+A_LAG = 4
+PROJECT_LAG = 5
 TURN_LEAD = 3
 WARM_UP = 9
 LOADS_AHEAD = 4
@@ -227,12 +227,14 @@ def tile_alibiattention_pa_t_kernel(tc, q, k, v, w_out, b_out, out):
                         stop=True,
                     )
 
-        def copy_qk(n):
+        def copy_qk(n, parts=1):
             turned_qk[n] = pools["turned_qk"].tile([P, 2, H, P], BF16, name="qk_t")
-            nc.scalar.copy(
-                out=turned_qk[n][:].rearrange("d w h r -> d (w h r)").bitcast(F32),
-                in_=qk_products[n][:].rearrange("d w h r -> d (w h r)").bitcast(F32),
-            )
+            target = turned_qk[n][:].rearrange("d w h r -> d (w h r)").bitcast(F32)
+            source = qk_products[n][:].rearrange("d w h r -> d (w h r)").bitcast(F32)
+            width = H * P // parts
+            for i in range(parts):
+                cols = slice(i * width, (i + 1) * width)
+                nc.scalar.copy(out=target[:, cols], in_=source[:, cols])
 
         jobs = [(n, i) for n in range(UNITS) for i in range(SETS[n % TILES])]
         scores, neg_maxima, exp_biases, row_sums, e_rows, turned_e, grouped_e, mx_e = {}, {}, {}, {}, {}, {}, {}, {}
@@ -507,7 +509,7 @@ def tile_alibiattention_pa_t_kernel(tc, q, k, v, w_out, b_out, out):
         lay_mask(1)
         for n in first_units[:2]:
             turn_qk(n)
-            copy_qk(n)
+            copy_qk(n, 2)
         add_scores(0)
         add_scores(1)
         for n in first_units[2:]:
@@ -545,6 +547,7 @@ def tile_alibiattention_pa_t_kernel(tc, q, k, v, w_out, b_out, out):
                 turn_w(2 * (r - 2))
             for j in jobs_now:
                 lay_mask(j + 2)
+            for j in jobs_now:
                 add_scores(j + 2)
             turn_e(r - 1)
             if r - 1 in product_at:
@@ -569,10 +572,10 @@ def tile_alibiattention_pa_t_kernel(tc, q, k, v, w_out, b_out, out):
             copy_e(r - 2)
             if r - 2 in product_at:
                 copy_a(product_at[r - 2])
-            if r > 0:
-                soften(2 * r)
             if r in turn_at:
                 copy_qk(turn_at[r])
+            if r > 0:
+                soften(2 * r)
             soften(2 * r + 1)
             if r in product_at and on_scalar(product_at[r]):
                 normalise(product_at[r])
@@ -586,7 +589,7 @@ def tile_alibiattention_pa_t_kernel(tc, q, k, v, w_out, b_out, out):
                     load_v(b)
 
         stages = (e_times_v, normalise, turn_a, copy_a, quantise_a, project, add_bias)
-        rounds_after = (0, 0, 1, 2, 3, 4, 4)
+        rounds_after = (0, 0, 1, 2, 4, 5, 5)
         left = {n: sum(r + after < PAIRS for after in rounds_after) for r, n in product_at.items()}
         copy_e(PAIRS - 2)
         turn_e(PAIRS - 1)

@@ -55,7 +55,7 @@ def last_job(n):
 
 
 def on_scalar(n):
-    return n % TILES == 3
+    return n % TILES == 3 or n % (2 * TILES) == TILES + 1
 
 
 def v_rounds(b):
@@ -90,17 +90,17 @@ def tile_alibiattention_pa_t_kernel(tc, q, k, v, w_out, b_out, out):
                 ("rows_qk", 7),
                 ("rows_v", 3),
                 ("turned_qk", 8),
-                ("maxima", 6),
-                ("sums", 8),
+                ("maxima", 24),
+                ("sums", 16),
                 ("e_rows", 4),
                 ("stage_e", 3),
-                ("stage", 3),
+                ("stage", 8),
                 ("stage_v", 2),
                 ("mx_e", 5),
                 ("mx_v", 2),
-                ("a_rows", 3),
-                ("mx_a", 5),
-                ("result", 4),
+                ("a_rows", 8),
+                ("mx_a", 10),
+                ("result", UNITS),
             )
         }
         pools["psum"] = stack.enter_context(tc.psum_pool(name="psum", bufs=PSUM_BANKS))
@@ -486,8 +486,13 @@ def tile_alibiattention_pa_t_kernel(tc, q, k, v, w_out, b_out, out):
                 return
             b, t = divmod(n, TILES)
             result = pools["result"].tile([P, D], F32)
-            nc.vector.tensor_tensor(out=result[:], in0=out_sums[n][:], in1=bias[:], op=ALU.add)
-            nc.sync.dma_start(out=out[b, t * P : (t + 1) * P, :], in_=result[:])
+            parts = 2 if n == UNITS - 1 else 1
+            for i in range(parts):
+                cols = slice(i * D // parts, (i + 1) * D // parts)
+                nc.vector.tensor_tensor(
+                    out=result[:, cols], in0=out_sums[n][:, cols], in1=bias[:, cols], op=ALU.add
+                )
+                nc.sync.dma_start(out=out[b, t * P : (t + 1) * P, cols], in_=result[:, cols])
 
         w_words = w_rows[:].bitcast(F32).rearrange("r t (u p) -> r t u p", u=2)
         turned_w = {}
@@ -537,12 +542,12 @@ def tile_alibiattention_pa_t_kernel(tc, q, k, v, w_out, b_out, out):
                     move_v_first(b)
                     move_v_two(b)
 
+            if r in turn_at:
+                turn_qk(turn_at[r])
             if r in product_at:
                 e_times_v(product_at[r])
             if r - PROJECT_LAG in product_at:
                 project(product_at[r - PROJECT_LAG])
-            if r in turn_at:
-                turn_qk(turn_at[r])
             if r in (2, 3):
                 turn_w(2 * (r - 2))
             for j in jobs_now:

@@ -574,14 +574,18 @@ def tile_alibiattention_pa_t_kernel(tc, q, k, v, w_out, b_out, out):
                     if r == v_rounds(b)[first // 2]:
                         group_v(b, first)
 
+            if r >= PAIRS - 1:
+                soften(2 * r)
+                soften(2 * r + 1)
             copy_e(r - 2)
             if r - 2 in product_at:
                 copy_a(product_at[r - 2])
             if r in turn_at:
                 copy_qk(turn_at[r])
-            if r > 0:
-                soften(2 * r)
-            soften(2 * r + 1)
+            if r < PAIRS - 1:
+                if r > 0:
+                    soften(2 * r)
+                soften(2 * r + 1)
             if r in product_at and on_scalar(product_at[r]):
                 normalise(product_at[r])
             if r in (2, 3):
@@ -603,7 +607,7 @@ def tile_alibiattention_pa_t_kernel(tc, q, k, v, w_out, b_out, out):
             quantise_e(p)
         invert(UNITS - 2)
         while min(left.values()) < len(stages):
-            for n in sorted(left):
+            for n in sorted(left, key=lambda n: (left[n] == 6, n)):
                 if left[n] < len(stages):
                     stages[left[n]](n)
                     left[n] += 1

import math
from contextlib import ExitStack

import concourse.mybir as mybir
from concourse.masks import make_identity

F32 = mybir.dt.float32
BF16 = mybir.dt.bfloat16
I32 = mybir.dt.int32
U32 = mybir.dt.uint32
U8 = mybir.dt.uint8
FP8X4 = mybir.dt.float8_e4m3fn_x4
ALU = mybir.AluOpType
FUNC = mybir.ActivationFunctionType
AXIS = mybir.AxisListType

B, H, S, HD = 8, 4, 512, 128
D = H * HD
P = 128
PACK = 4
TILES = S // P
HALF = S // 2
Q_PARTS = P // PACK
UNITS = B * TILES
NEG_INF = -1e30
ROOT = math.sqrt(HD)

QUADRANT = ((0, 1, 2, 3), (2, 3, 1, 0), (1, 0, 2, 3), (3, 2, 1, 0))
SETS = (1, 2, 4, 4)
SEQ_JOBS = sum(SETS)
JOBS = B * SEQ_JOBS
PAIRS = JOBS // 2
TWO_SEQ_PAIRS = SEQ_JOBS
V_STEPS = ((-5, -3, -1), (1, 2, 6))
V_LOAD_LEAD = 4
PSUM_BANKS = 8
QUANTISE_LAG = 3
PRODUCT_LAG = 3
A_LAG = 4
PROJECT_LAG = 5
TURN_LEAD = 3
WARM_UP = 9
LOADS_AHEAD = 4

FLOPS = 2 * (2 * B * H * S * S * HD) + 2 * B * S * D * D


def first_quadrant(h, t):
    return min(QUADRANT[h][: t + 1])


def last_job(n):
    b, t = divmod(n, TILES)
    return SEQ_JOBS * b + sum(SETS[: t + 1]) - 1


def on_scalar(n):
    return n % TILES == 3 or n % (2 * TILES) == TILES + 1


def v_rounds(b):
    return ((1, 2, 3), (3, 4, 6))[b] if b < 2 else tuple(TWO_SEQ_PAIRS * (b // 2) + step for step in V_STEPS[b % 2])


def product_rounds():
    rounds = []
    for n in range(UNITS):
        earliest = last_job(n) // 4 * 2 + 1 + PRODUCT_LAG
        rounds.append(max(earliest, rounds[-1] + 1) if rounds else earliest)
    return rounds


def turn_rounds():
    rounds = []
    for n in reversed(range(UNITS)):
        first_job = last_job(n) - SETS[n % TILES] + 1
        r = min([first_job // 2 - TURN_LEAD] + [later - 1 for later in rounds[-1:]])
        rounds.append(r - (r > 0 and r % TWO_SEQ_PAIRS == 0))
    return rounds[::-1]


def tile_alibiattention_pa_t_kernel(tc, q, k, v, w_out, b_out, out):
    nc = tc.nc
    with ExitStack() as stack:
        stack.enter_context(tc.manual_schedule())
        pools = {
            name: stack.enter_context(tc.tile_pool(name=name, bufs=bufs))
            for name, bufs in (
                ("consts", 1),
                ("rows_qk", 7),
                ("rows_v", 3),
                ("turned_qk", 8),
                ("maxima", 24),
                ("sums", 16),
                ("e_rows", 4),
                ("stage_e", 3),
                ("stage", 8),
                ("stage_v", 2),
                ("mx_e", 5),
                ("mx_v", 2),
                ("a_rows", 8),
                ("mx_a", 10),
                ("result", UNITS),
            )
        }
        pools["psum"] = stack.enter_context(tc.psum_pool(name="psum", bufs=PSUM_BANKS))
        consts = pools["consts"]

        rows_qk, rows_v = {}, {}

        def load_qk(n):
            if n >= UNITS:
                return
            b, t = divmod(n, TILES)
            rows = pools["rows_qk"].tile([P, 2, H, HD], BF16)
            for which, source in enumerate((q, k)):
                nc.sync.dma_start(
                    out=rows[:, which, :, :],
                    in_=source[b, :, t * P : (t + 1) * P, :].rearrange("h r d -> r h d"),
                )
            rows_qk[n] = rows

        def load_v(b):
            if b >= B:
                return
            rows = pools["rows_v"].tile([P, H, PACK, HD], BF16)
            for h in range(H):
                m = 0
                while m < TILES:
                    after = m + 1
                    while after < TILES and QUADRANT[h][after] == QUADRANT[h][after - 1] + 1:
                        after += 1
                    part = QUADRANT[h][m] * Q_PARTS
                    nc.sync.dma_start(
                        out=rows[part : part + (after - m) * Q_PARTS, h, :, :],
                        in_=v[b, h, m * P : after * P, :].rearrange("(p c) d -> p c d", c=PACK),
                    )
                    m = after
            rows_v[b] = rows

        for n in range(LOADS_AHEAD):
            load_qk(n)
        load_v(0)
        load_qk(LOADS_AHEAD)
        w_rows = consts.tile([P, TILES, D], BF16)
        nc.sync.dma_start(out=w_rows[:], in_=w_out.rearrange("(t r) c -> r t c", r=P))
        load_qk(LOADS_AHEAD + 1)
        load_qk(LOADS_AHEAD + 2)
        bias = consts.tile([P, D], BF16)
        nc.sync.dma_start(out=bias[:], in_=b_out.partition_broadcast(P))
        load_v(1)

        distance = consts.tile([P, TILES, P], I32)
        alibi = consts.tile([P, TILES, P], F32)
        ident_f32 = consts.tile([P, P], F32)
        ident_bf16 = consts.tile([P, P], BF16)
        make_identity(nc, ident_bf16[:])
        nc.gpsimd.iota(distance[:, 0, :], pattern=[[-1, P]], base=0, channel_multiplier=1)
        make_identity(nc, ident_f32[:])
        nc.gpsimd.iota(distance[:, 1:, :], pattern=[[-P, TILES - 1], [-1, P]], base=-P, channel_multiplier=1)
        future = consts.tile([P, P], F32)
        nc.vector.tensor_scalar(
            out=future[:],
            in0=distance[:, 0, :],
            scalar1=0.0,
            scalar2=ROOT * NEG_INF,
            op0=ALU.is_gt,
            op1=ALU.mult,
        )
        nc.vector.scalar_tensor_tensor(
            out=alibi[:, 0, :],
            in0=distance[:, 0, :],
            scalar=ROOT,
            in1=future[:],
            op0=ALU.mult,
            op1=ALU.add,
        )
        nc.vector.tensor_scalar(
            out=alibi[:, 1:, :], in0=distance[:, 1:, :], scalar1=ROOT, scalar2=None, op0=ALU.mult
        )

        zero = consts.tile([P, 1], F32)
        nc.vector.memset(zero[:], 0.0)
        one = consts.tile([P, 1], F32)
        nc.scalar.activation(out=one[:], in_=zero[:], func=FUNC.Exp)

        e_rows_three = [consts.tile([P, 2, HALF], BF16, name="e_rows_three%d" % h) for h in range(H)]
        v_first = [consts.tile([P, H, HD], U32, align_bytes=64, name="v_first%d" % i) for i in range(2)]
        v_two = [consts.tile([P, H, HD], U32, align_bytes=64, name="v_two%d" % i) for i in range(2)]

        def lay_zeros_e():
            for h in range(H):
                low = QUADRANT[h][TILES - 1] * 2 * Q_PARTS
                nc.vector.memset(e_rows_three[h][:, :, low : low + 2 * Q_PARTS], 0.0)

        def lay_zeros_v(b):
            for codes in (v_first[b % 2], v_two[b % 2]):
                nc.vector.memset(codes[:].bitcast(I32), 0)

        def turn_words(turned, words):
            for u in range(2):
                nc.tensor.transpose(turned[:, u, :], words[:, u, :], ident_f32[:])

        def group_words(turned, grouped):
            nc.scalar.copy(out=grouped.bitcast(F32), in_=turned[:].rearrange("p t u r -> p t r u"))

        def quantise(grouped, keep):
            columns = grouped.shape[1]
            codes = keep.tile([P, columns], U32, align_bytes=64)
            scales = keep.tile([P, columns], U8, align_bytes=64)
            nc.vector.quantize_mx(
                out=codes[:].bitcast(FP8X4), scales=scales[:], in_=grouped.rearrange("p n c -> p (n c)")
            )
            return codes, scales

        qk_products, turned_qk = {}, {}

        def turn_qk(n):
            qk_products[n] = pools["psum"].tile([P, 2, H, P], BF16, name="bank")
            for which in range(2):
                for h in range(H):
                    nc.tensor.matmul(
                        qk_products[n][:, which, h, :],
                        lhsT=rows_qk[n][:, which, h, :],
                        rhs=ident_bf16[:],
                        start=True,
                        stop=True,
                    )

        def copy_qk(n, parts=1):
            turned_qk[n] = pools["turned_qk"].tile([P, 2, H, P], BF16, name="qk_t")
            target = turned_qk[n][:].rearrange("d w h r -> d (w h r)").bitcast(F32)
            source = qk_products[n][:].rearrange("d w h r -> d (w h r)").bitcast(F32)
            width = H * P // parts
            for i in range(parts):
                cols = slice(i * width, (i + 1) * width)
                nc.scalar.copy(out=target[:, cols], in_=source[:, cols])

        jobs = [(n, i) for n in range(UNITS) for i in range(SETS[n % TILES])]
        scores, neg_maxima, exp_biases, row_sums, e_rows, turned_e, grouped_e, mx_e = {}, {}, {}, {}, {}, {}, {}, {}

        def job_heads(j):
            n, i = jobs[j]
            heads = H // SETS[n % TILES]
            return n, n % TILES, range(i * heads, (i + 1) * heads)

        def lay_mask(j):
            if not 0 <= j < JOBS:
                return
            n, t, heads = job_heads(j)
            keys = (t + 1) * P
            scores[j] = pools["psum"].tile([P, S], F32, name="bank")
            for i, h in enumerate(heads):
                for place in range(t + 1):
                    m = QUADRANT[h].index(first_quadrant(h, t) + place)
                    nc.tensor.matmul(
                        scores[j][:, i * keys + place * P : i * keys + (place + 1) * P],
                        lhsT=alibi[:, t - m, :],
                        rhs=ident_f32[:],
                        start=i == 0 and place == 0,
                        stop=False,
                        is_transpose=True,
                    )

        def add_scores(j):
            if not 0 <= j < JOBS:
                return
            n, t, heads = job_heads(j)
            for i, h in enumerate(heads):
                for place in range(t + 1):
                    m = QUADRANT[h].index(first_quadrant(h, t) + place)
                    block = i * (t + 1) + place
                    nc.tensor.matmul(
                        scores[j][:, block * P : (block + 1) * P],
                        lhsT=turned_qk[n][:, 0, h, :],
                        rhs=turned_qk[n - t + m][:, 1, h, :],
                        start=False,
                        stop=h == heads[-1] and place == t,
                    )

        def row_max(j):
            if not 0 <= j < JOBS:
                return
            n, t, heads = job_heads(j)
            keys = (t + 1) * P
            neg_max = pools["maxima"].tile([P, len(heads)], F32, name="neg_max")
            nc.vector.tensor_reduce(
                out=neg_max[:],
                in_=scores[j][:, : len(heads) * keys].rearrange("r (h j) -> r h j", j=keys),
                axis=AXIS.X,
                op=ALU.max,
                negate=True,
            )
            neg_maxima[j] = neg_max

        def scale_max(j):
            if not 0 <= j < JOBS:
                return
            exp_biases[j] = pools["maxima"].tile([P, len(job_heads(j)[2])], F32, name="exp_bias")
            nc.gpsimd.tensor_scalar(
                out=exp_biases[j][:],
                in0=neg_maxima[j][:],
                scalar1=1.0 / ROOT,
                scalar2=0.0,
                op0=ALU.mult,
                op1=ALU.add,
            )

        def soften(j):
            if not 0 <= j < JOBS:
                return
            n, t, heads = job_heads(j)
            keys = (t + 1) * P
            if heads[0] == 0 and n % 2 == 0:
                row_sum = pools["sums"].tile([P, 2, H], F32, name="row_sum")
                row_sums[n], row_sums[n + 1] = row_sum[:, 0, :], row_sum[:, 1, :]
                pair_sums[n] = row_sum
            if t == 2:
                e_rows[j] = e_rows_three[heads[0]]
            else:
                e_rows[j] = pools["e_rows"].tile([P, 2, HALF], BF16, name="e_rows")
            for i, h in enumerate(heads):
                low = first_quadrant(h, t) * 2 * Q_PARTS
                nc.scalar.activation(
                    out=e_rows[j][:, :, low : low + keys // 2].rearrange("r u (p x) -> r u p x", x=2),
                    in_=scores[j][:, i * keys : (i + 1) * keys].rearrange(
                        "r (p u x) -> r u p x", u=2, x=2
                    ),
                    func=FUNC.Exp,
                    bias=exp_biases[j][:, i : i + 1],
                    scale=1.0 / ROOT,
                    accum_out=row_sums[n][:, h : h + 1],
                )

        def turn_e(p):
            if not 0 <= p < PAIRS:
                return
            turned_e[p] = pools["psum"].tile([P, 2, 2, P], F32, name="bank")
            for i in range(2):
                turn_words(turned_e[p][:, i], e_rows[2 * p + i][:].bitcast(F32))

        def copy_e(p):
            if not 0 <= p < PAIRS:
                return
            if p % 2 == 0:
                grouped_e[p // 2] = pools["stage_e"].tile([P, 4, P, PACK], BF16, align_bytes=64, name="grouped_e")
            half = slice(p % 2 * 2, p % 2 * 2 + 2)
            group_words(turned_e[p], grouped_e[p // 2][:, half])

        def quantise_e(p):
            if not 0 <= p < PAIRS or p % 2 == 0:
                return
            codes, scales = quantise(grouped_e[p // 2][:].rearrange("p t r c -> p (t r) c"), pools["mx_e"])
            for i in range(4):
                mx_e[2 * p - 2 + i] = (codes[:, i * P : (i + 1) * P], scales[:, i * P : (i + 1) * P])

        grouped_v, mx_v = {}, {}

        def group_v(b, first):
            if b >= B:
                return
            if first == 0:
                grouped_v[b] = pools["stage_v"].tile(
                    [P, H, HD, PACK], BF16, align_bytes=64, name="grouped_v"
                )
            heads = slice(first, first + 2)
            nc.vector.tensor_copy(
                out=grouped_v[b][:, heads, :, :].rearrange("p h (d i) c -> p h d c i", i=PACK),
                in_=rows_v[b][:, heads, :, :].rearrange("p h c (d i) -> p h d c i", i=PACK),
            )

        def quantise_v(b):
            if b >= B:
                return
            mx_v[b] = quantise(grouped_v[b][:].rearrange("p h d c -> p (h d) c"), pools["mx_v"])

        def move_v_two(b):
            if b >= B:
                return
            codes = mx_v[b][0][:].rearrange("p (h d) -> p h d", h=H).bitcast(I32)
            two = v_two[b % 2][:].bitcast(I32)
            move = nc.sync.dma_start if b > 0 else nc.vector.tensor_copy
            for low in range(2):
                part = slice(low * P // 2, (low + 1) * P // 2)
                move(out=two[part, low::2, :], in_=codes[part, low::2, :])

        def move_v_first(b):
            if b >= B:
                return
            codes = mx_v[b][0][:].rearrange("p (h d) -> p h d", h=H).bitcast(I32)
            one_block = v_first[b % 2][:].bitcast(I32)
            move = nc.sync.dma_start if b > 0 else nc.vector.tensor_copy
            for h in range(H):
                low = QUADRANT[h][0] * Q_PARTS
                part = slice(low, low + Q_PARTS)
                move(out=one_block[part, h, :], in_=codes[part, h, :])

        pair_sums, heads_sums, inverse_sums, a_rows, turned_a, grouped_a, mx_a, out_sums = {}, {}, {}, {}, {}, {}, {}, {}

        def e_times_v(n):
            if not 0 <= n < UNITS:
                return
            b, t = divmod(n, TILES)
            v_codes, v_scales = mx_v[b]
            if t == 0:
                v_codes = v_first[b % 2][:].rearrange("p h d -> p (h d)")
            elif t == 1:
                v_codes = v_two[b % 2][:].rearrange("p h d -> p (h d)")
            else:
                v_codes = v_codes[:]
            o_sums = pools["psum"].tile([P, D], F32, name="bank")
            width = D // SETS[t]
            for i in range(SETS[t]):
                e_codes, e_scales = mx_e[last_job(n) - SETS[t] + 1 + i]
                v_cols = slice(i * width, (i + 1) * width)
                nc.tensor.matmul_mx(
                    out=o_sums[:, v_cols],
                    lhsT=e_codes.bitcast(FP8X4),
                    lhsT_scale=e_scales,
                    rhs=v_codes[:, v_cols].bitcast(FP8X4),
                    rhs_scale=v_scales[:, v_cols],
                    start=True,
                    stop=True,
                )
            heads_sums[n] = o_sums

        def invert(n):
            one_over_sum = pools["sums"].tile([P, 2, H], F32)
            nc.vector.reciprocal(out=one_over_sum[:], in_=pair_sums[n][:])
            inverse_sums[n], inverse_sums[n + 1] = one_over_sum[:, 0, :], one_over_sum[:, 1, :]

        def normalise(n):
            if not 0 <= n < UNITS:
                return
            a_rows[n] = pools["a_rows"].tile([P, 2, HALF], BF16, name="a_rows")
            if on_scalar(n):
                for h in range(H):
                    nc.scalar.activation(
                        out=a_rows[n][:].rearrange("r u c -> r (u c)")[:, h * HD : (h + 1) * HD],
                        in_=heads_sums[n][:, h * HD : (h + 1) * HD],
                        func=FUNC.Copy,
                        scale=inverse_sums[n][:, h : h + 1],
                    )
                return
            nc.vector.tensor_tensor(
                out=a_rows[n][:].rearrange("r u c -> r (u c)").rearrange("r (h d) -> r h d", h=H),
                in0=heads_sums[n][:].rearrange("r (h d) -> r h d", h=H),
                in1=inverse_sums[n].unsqueeze(2).to_broadcast([P, H, HD]),
                op=ALU.mult,
            )

        def turn_a(n):
            if not 0 <= n < UNITS:
                return
            turned_a[n] = pools["psum"].tile([P, 1, 2, P], F32, name="bank")
            turn_words(turned_a[n][:, 0], a_rows[n][:].bitcast(F32))

        def copy_a(n):
            if not 0 <= n < UNITS:
                return
            grouped_a[n] = pools["stage"].tile([P, 1, P, PACK], BF16, align_bytes=64, name="grouped_a")
            group_words(turned_a[n], grouped_a[n][:])

        def quantise_a(n):
            if not 0 <= n < UNITS:
                return
            mx_a[n] = quantise(grouped_a[n][:].rearrange("p t r c -> p (t r) c"), pools["mx_a"])

        def project(n):
            if not 0 <= n < UNITS:
                return
            a_codes, a_scales = mx_a[n]
            out_sums[n] = pools["psum"].tile([P, D], F32, name="bank")
            nc.tensor.matmul_mx(
                out=out_sums[n][:],
                lhsT=a_codes[:].bitcast(FP8X4),
                lhsT_scale=a_scales[:],
                rhs=w_codes[0][:].bitcast(FP8X4),
                rhs_scale=w_scales[0][:],
                start=True,
                stop=True,
            )

        def add_bias(n):
            if not 0 <= n < UNITS:
                return
            b, t = divmod(n, TILES)
            result = pools["result"].tile([P, D], F32)
            parts = 2 if n == UNITS - 1 else 1
            for i in range(parts):
                cols = slice(i * D // parts, (i + 1) * D // parts)
                nc.vector.tensor_tensor(
                    out=result[:, cols], in0=out_sums[n][:, cols], in1=bias[:, cols], op=ALU.add
                )
                nc.sync.dma_start(out=out[b, t * P : (t + 1) * P, cols], in_=result[:, cols])

        w_words = w_rows[:].bitcast(F32).rearrange("r t (u p) -> r t u p", u=2)
        turned_w = {}
        grouped_w = consts.tile([P, TILES, P, PACK], BF16, align_bytes=64)
        w_codes, w_scales = [], []

        def turn_w(first):
            turned_w[first] = pools["psum"].tile([P, 2, 2, P], F32, name="bank")
            for i in range(2):
                turn_words(turned_w[first][:, i], w_words[:, first + i])

        product_at = {r: n for n, r in enumerate(product_rounds())}
        turn_at = {r: n for n, r in enumerate(turn_rounds())}
        warm = pools["psum"].tile([P, TILES, P], F32, name="bank")
        for i in range(WARM_UP):
            nc.tensor.matmul(warm[:, i % TILES, :], lhsT=ident_bf16[:], rhs=ident_bf16[:], start=True, stop=True)
        first_units = [n for r, n in sorted(turn_at.items()) if r < 0]
        lay_mask(0)
        lay_mask(1)
        for n in first_units[:2]:
            turn_qk(n)
            copy_qk(n, 2)
        add_scores(0)
        add_scores(1)
        for n in first_units[2:]:
            turn_qk(n)
        lay_zeros_e()
        lay_zeros_v(0)
        lay_zeros_v(1)
        row_max(0)
        scale_max(0)
        soften(0)
        for n in first_units[2:]:
            copy_qk(n)
        for r in range(PAIRS):
            jobs_now = (2 * r, 2 * r + 1)
            quantise_e(r - QUANTISE_LAG)
            if r - A_LAG in product_at:
                quantise_a(product_at[r - A_LAG])
            if r == 5:
                codes, scales = quantise(grouped_w[:].rearrange("p t r c -> p (t r) c"), consts)
                w_codes.append(codes)
                w_scales.append(scales)
            for b in range(B):
                if r == v_rounds(b)[2]:
                    quantise_v(b)
                    move_v_first(b)
                    move_v_two(b)

            if r in turn_at:
                turn_qk(turn_at[r])
            if r in product_at:
                e_times_v(product_at[r])
            if r - PROJECT_LAG in product_at:
                project(product_at[r - PROJECT_LAG])
            if r in (2, 3):
                turn_w(2 * (r - 2))
            for j in jobs_now:
                lay_mask(j + 2)
            for j in jobs_now:
                add_scores(j + 2)
            turn_e(r - 1)
            if r - 1 in product_at:
                turn_a(product_at[r - 1])

            for j in jobs_now:
                if j > 0:
                    row_max(j)
                    scale_max(j)
            for n in range(0, UNITS, 2):
                if last_job(n + 1) // 2 == r - 1:
                    invert(n)
            if r in product_at and not on_scalar(product_at[r]):
                normalise(product_at[r])
            if r - PROJECT_LAG in product_at:
                add_bias(product_at[r - PROJECT_LAG])
            for b in range(B):
                for first in (0, 2):
                    if r == v_rounds(b)[first // 2]:
                        group_v(b, first)

            if r >= PAIRS - 1:
                soften(2 * r)
                soften(2 * r + 1)
            copy_e(r - 2)
            if r - 2 in product_at:
                copy_a(product_at[r - 2])
            if r in turn_at:
                copy_qk(turn_at[r])
            if r < PAIRS - 1:
                if r > 0:
                    soften(2 * r)
                soften(2 * r + 1)
            if r in product_at and on_scalar(product_at[r]):
                normalise(product_at[r])
            if r in (2, 3):
                group_words(turned_w[2 * (r - 2)], grouped_w[:, 2 * (r - 2) : 2 * (r - 1)])

            if r in turn_at:
                load_qk(turn_at[r] + LOADS_AHEAD)
            for b in range(B):
                if r == v_rounds(b)[0] - V_LOAD_LEAD and b > 1:
                    load_v(b)

        stages = (e_times_v, normalise, turn_a, copy_a, quantise_a, project, add_bias)
        rounds_after = (0, 0, 1, 2, 4, 5, 5)
        left = {n: sum(r + after < PAIRS for after in rounds_after) for r, n in product_at.items()}
        copy_e(PAIRS - 2)
        turn_e(PAIRS - 1)
        copy_e(PAIRS - 1)
        for p in range(PAIRS - QUANTISE_LAG, PAIRS):
            quantise_e(p)
        invert(UNITS - 2)
        while min(left.values()) < len(stages):
            for n in sorted(left, key=lambda n: (left[n] == 6, n)):
                if left[n] < len(stages):
                    stages[left[n]](n)
                    left[n] += 1
